import numpy as np
import ml_dtypes


def mxq(x, axis, fmt="e4m3"):
    dtype, down = {"e4m3": (ml_dtypes.float8_e4m3fn, 7), "e5m2": (ml_dtypes.float8_e5m2, 14)}[fmt]
    v = np.moveaxis(np.asarray(x, np.float32).astype(ml_dtypes.bfloat16).astype(np.float64), axis, -1)
    blocks = v.reshape(v.shape[:-1] + (-1, 32))
    amax = np.abs(blocks).max(-1, keepdims=True)
    byte = np.maximum(np.where(amax > 0, np.frexp(amax)[1] - 1 + 127, 0) - down, 1)
    scale = np.exp2(byte - 127.0)
    codes = (blocks / scale).astype(np.float32).astype(dtype).astype(np.float64)
    return np.moveaxis((codes * scale).reshape(v.shape), -1, axis)


WIDE = False


def mx_kscale(k):
    if not WIDE:
        return np.ones(k)
    levels = np.array([10, -10, 5, -5, 0])
    a = np.random.permutation(np.resize(levels, k // 512 * 4)).reshape(k // 512, 4)
    idx = np.arange(k)
    return np.exp2(a[idx // 512, idx % 128 // 32])


BF16 = ml_dtypes.bfloat16


def bf(x):
    return np.asarray(x, np.float32).astype(BF16)


def f64(x):
    return np.asarray(x).astype(np.float64)


B, L, D, F = 2, 512, 1024, 1536


def silu(z):
    return z / (1.0 + np.exp(-z))


def sigmoid(z):
    return 1.0 / (1.0 + np.exp(-z))


def setup_inputs():
    s = mx_kscale(D)
    return {
        "x": bf(np.random.standard_normal((B, L, D)) * s),
        "W1": bf(np.random.standard_normal((D, F)) / np.sqrt(D) / s[:, None]),
        "b1": bf(np.random.standard_normal(F) * 0.3),
        "W2g": bf(np.random.standard_normal((F, D)) * 2.4 / np.sqrt(F)),
        "b2g": bf(np.random.standard_normal(D) * 0.3),
        "Wv": bf(np.random.standard_normal((D, D)) * 1.8 / np.sqrt(D) / s[:, None]),
        "bv": bf(np.random.standard_normal(D) * 0.3),
    }


def reference(x, W1, b1, W2g, b2g, Wv, bv):
    xq = mxq(f64(x), 2, "e4m3")
    h = silu((xq @ mxq(f64(W1), 0, "e4m3")) + f64(b1))
    g = (mxq(h, 2, "e4m3") @ mxq(f64(W2g), 0, "e4m3")) + f64(b2g)
    return ((xq @ mxq(f64(Wv), 0, "e4m3")) + f64(bv)) * sigmoid(g)

@@ -1,0 +1,230 @@
+from contextlib import ExitStack
+
+import concourse.masks as masks
+import concourse.mybir as mybir
+
+FLOPS = 2 * 1024 * (1024 * 1536 + 1536 * 1024 + 1024 * 1024)
+
+F32 = mybir.dt.float32
+BF16 = mybir.dt.bfloat16
+U32 = mybir.dt.uint32
+U8 = mybir.dt.uint8
+FP8X4 = mybir.dt.float8_e4m3fn_x4
+ACT = mybir.ActivationFunctionType
+ALU = mybir.AluOpType
+
+P = 128
+CH = 512
+
+
+def tile_selectivemixing_pa_kernel(tc, x, W1, b1, W2g, b2g, Wv, bv, out):
+    nc = tc.nc
+    with ExitStack() as ctx:
+        const = ctx.enter_context(tc.tile_pool(name="const", bufs=1))
+        keep = ctx.enter_context(tc.tile_pool(name="keep", bufs=1))
+        stage = ctx.enter_context(tc.tile_pool(name="stage", bufs=6))
+        tail = ctx.enter_context(tc.tile_pool(name="tail", bufs=3))
+        ps_acc = ctx.enter_context(tc.psum_pool(name="acc", bufs=4))
+        ps_tr = ctx.enter_context(tc.psum_pool(name="tr", bufs=4))
+
+        ident_f = const.tile([P, P], F32, name="ident_f")
+        masks.make_identity(nc, ident_f[:])
+        ident_b = const.tile([P, P], BF16, name="ident_b")
+        masks.make_identity(nc, ident_b[:])
+        brow = const.tile([P, P], BF16, name="brow")
+        nc.vector.memset(brow[:], 0.0)
+        warm = const.tile([P, 4], F32, name="warm")
+        nc.vector.memset(warm[:], 0.0)
+        nc.scalar.activation(out=warm[:, 1:2], in_=warm[:, 0:1], func=ACT.Silu)
+        nc.scalar.dma_start(out=brow[0:12, :], in_=b1.rearrange("(j p) -> j p", p=P))
+        nc.scalar.dma_start(out=brow[12:20, :], in_=b2g.rearrange("(j p) -> j p", p=P))
+        nc.scalar.dma_start(out=brow[20:28, :], in_=bv.rearrange("(j p) -> j p", p=P))
+
+        xv = x.flatten_outer_dims().rearrange("(p i) k -> p i k", i=8)
+        ov = out.flatten_outer_dims().rearrange("(p i) d -> p i d", i=8)
+        x_sb = {}
+        raw = {}
+
+        def load_x(q):
+            t = keep.tile([P, 2, 1024], BF16, name="x_%d" % q)
+            nc.sync.dma_start(out=t[:], in_=xv[:, 2 * q : 2 * q + 2, :])
+            x_sb[q] = t
+
+        def load_pairs(W, nm, ch, g):
+            view = W.rearrange("(a p e) f -> e p a f", a=4, p=P, e=2)
+            t = keep.tile([P, 4, CH], BF16, name="r_%s_%d_%d" % (nm, ch, g))
+            tv = t[:].rearrange("p (u e) f -> p u e f", e=2)
+            for e in range(2):
+                nc.sync.dma_start(
+                    out=tv[:, :, e, :],
+                    in_=view[e, :, 2 * g : 2 * g + 2, ch * CH : (ch + 1) * CH],
+                )
+            raw[(nm, ch, g)] = t
+
+        def load_rows(W, nm, ch, g):
+            view = W.rearrange("(g t p) n -> g p t n", g=3, t=4, p=P)
+            t = keep.tile([P, 4, CH], BF16, name="r_%s_%d_%d" % (nm, ch, g))
+            nc.sync.dma_start(out=t[:], in_=view[g, :, :, ch * CH : (ch + 1) * CH])
+            raw[(nm, ch, g)] = t
+
+        load_x(0)
+        load_x(1)
+        load_pairs(W1, "w1", 0, 0)
+        load_pairs(W1, "w1", 0, 1)
+        load_x(2)
+        load_x(3)
+        for ch in (1, 2):
+            for g in range(2):
+                load_pairs(W1, "w1", ch, g)
+        for ch in range(2):
+            for g in range(2):
+                load_pairs(Wv, "wv", ch, g)
+            for g in range(3):
+                load_rows(W2g, "w2", ch, g)
+
+        bt = ps_tr.tile([P, P], BF16, name="bt", tag="tr")
+        nc.tensor.transpose(bt[:], brow[:], ident_b[:])
+        bcol = const.tile([P, 32], F32, name="bcol")
+        nc.vector.tensor_copy(out=bcol[:, 0:28], in_=bt[:, 0:28])
+
+        q = {}
+
+        def regroup(eng, src):
+            grp = stage.tile([P, CH, 4], BF16, name="grp", tag="grp", align_bytes=64)
+            o = grp[:].rearrange("p (c i) t -> p c t i", i=4)
+            s = src[:].rearrange("p t (c i) -> p c t i", i=4)
+            if eng == "v":
+                nc.vector.tensor_copy(out=o, in_=s)
+            else:
+                nc.scalar.copy(out=o, in_=s)
+            return grp
+
+        def quantise(grp, key):
+            nm = "%s_%d_%d" % key
+            codes = keep.tile([P, CH], U32, name="c_" + nm, align_bytes=64)
+            scales = keep.tile([P, CH], U8, name="s_" + nm, align_bytes=64)
+            nc.vector.quantize_mx(
+                out=codes[:].bitcast(FP8X4),
+                scales=scales[:],
+                in_=grp[:].rearrange("p w j -> p (w j)"),
+            )
+            q[key] = (codes, scales)
+
+        def prep(jobs):
+            pending = None
+            for eng, src, key in jobs:
+                grp = regroup(eng, src)
+                if pending is not None:
+                    quantise(pending[0], pending[1])
+                pending = (grp, key)
+            quantise(pending[0], pending[1])
+
+        def mx(acc, wkey, col, xkey, start, stop):
+            wc, ws = q[wkey]
+            xc, xs = q[xkey]
+            nc.tensor.matmul_mx(
+                out=acc[:],
+                lhsT=wc[:, col * P : (col + 1) * P].bitcast(FP8X4),
+                lhsT_scale=ws[:, col * P : (col + 1) * P],
+                rhs=xc[:].bitcast(FP8X4),
+                rhs_scale=xs[:],
+                start=start,
+                stop=stop,
+            )
+
+        def x_half(c):
+            grps = {}
+            for g in range(2):
+                grps[g] = stage.tile([P, CH, 4], BF16, name="gx", tag="grp", align_bytes=64)
+            for qq in range(2):
+                xw = x_sb[2 * c + qq][:].bitcast(F32)
+                for g in range(2):
+                    xt = ps_tr.tile([P, 2, 256], F32, name="xt", tag="tr")
+                    for u in range(2):
+                        for ii in range(2):
+                            lo = 256 * g + 128 * u
+                            nc.tensor.transpose(
+                                xt[:, u, ii * P : (ii + 1) * P], xw[:, ii, lo : lo + P], ident_f[:]
+                            )
+                    nc.scalar.copy(
+                        out=grps[g][:].bitcast(F32)[:, 256 * qq : 256 * qq + 256, :],
+                        in_=xt[:].rearrange("p u r -> p r u"),
+                    )
+            return grps
+
+        gx0 = x_half(0)
+        prep([("v", raw[("w1", 0, 0)], ("w1", 0, 0)), ("v", raw[("w1", 0, 1)], ("w1", 0, 1))])
+        quantise(gx0[0], ("x", 0, 0))
+        quantise(gx0[1], ("x", 1, 0))
+        gx1 = x_half(1)
+        prep([("v", raw[("w1", 1, 0)], ("w1", 1, 0)), ("v", raw[("w1", 1, 1)], ("w1", 1, 1))])
+        quantise(gx1[0], ("x", 0, 1))
+        quantise(gx1[1], ("x", 1, 1))
+        prep([("v", raw[("w1", 2, 0)], ("w1", 2, 0)), ("v", raw[("w1", 2, 1)], ("w1", 2, 1))])
+
+        hT = {}
+        for fc in range(3):
+            for c in range(2):
+                hT[(fc, c)] = keep.tile([P, 4, CH], BF16, name="h_%d_%d" % (fc, c))
+            for jj in range(4):
+                for c in range(2):
+                    z = ps_acc.tile([P, CH], F32, name="z", tag="acc")
+                    for g in range(2):
+                        mx(z, ("w1", fc, g), jj, ("x", g, c), g == 0, g == 1)
+                    j = 4 * fc + jj
+                    nc.scalar.activation(
+                        out=hT[(fc, c)][:, jj, :], in_=z[:], func=ACT.Silu,
+                        bias=bcol[:, j : j + 1], scale=1.0,
+                    )
+            prep([("v", hT[(fc, 0)], ("h", fc, 0)), ("v", hT[(fc, 1)], ("h", fc, 1))])
+        nc.scalar.activation(out=warm[:, 2:3], in_=hT[(2, 1)][:, 3, 0:1], func=ACT.Sigmoid)
+
+        prep([
+            ("s", raw[("wv", 0, 0)], ("wv", 0, 0)),
+            ("v", raw[("w2", 0, 0)], ("w2", 0, 0)),
+            ("s", raw[("wv", 0, 1)], ("wv", 0, 1)),
+            ("v", raw[("w2", 0, 1)], ("w2", 0, 1)),
+            ("v", raw[("w2", 0, 2)], ("w2", 0, 2)),
+        ])
+        late = [
+            [("v", raw[("w2", 1, 0)], ("w2", 1, 0)), ("v", raw[("w2", 1, 1)], ("w2", 1, 1))],
+            [("v", raw[("w2", 1, 2)], ("w2", 1, 2)), ("v", raw[("wv", 1, 0)], ("wv", 1, 0))],
+            [("v", raw[("wv", 1, 1)], ("wv", 1, 1))],
+        ]
+
+        oT = {}
+
+        def finish(j):
+            for c in range(2):
+                ot = ps_tr.tile([P, 4, P], F32, name="ot", tag="tr")
+                for r in range(4):
+                    nc.tensor.transpose(ot[:, r, :], oT[(j, c)][:, r * P : (r + 1) * P], ident_f[:])
+                o_sb = tail.tile([P, 4, P], F32, name="o_sb", tag="o_sb")
+                nc.scalar.copy(out=o_sb[:], in_=ot[:])
+                nc.sync.dma_start(out=ov[:, 4 * c : 4 * c + 4, j * P : (j + 1) * P], in_=o_sb[:])
+
+        for j in range(8):
+            half, col = j // 4, j % 4
+            for c in range(2):
+                gps = ps_acc.tile([P, CH], F32, name="gps", tag="acc")
+                for g in range(3):
+                    mx(gps, ("w2", half, g), col, ("h", g, c), g == 0, g == 2)
+                vps = ps_acc.tile([P, CH], F32, name="vps", tag="acc")
+                for g in range(2):
+                    mx(vps, ("wv", half, g), col, ("x", g, c), g == 0, g == 1)
+                s_sb = tail.tile([P, CH], F32, name="s_sb", tag="s_sb")
+                nc.scalar.activation(
+                    out=s_sb[:], in_=gps[:], func=ACT.Sigmoid,
+                    bias=bcol[:, 12 + j : 13 + j], scale=1.0,
+                )
+                o_t = tail.tile([P, CH], F32, name="o_t", tag="o_t", bufs=4)
+                nc.vector.scalar_tensor_tensor(
+                    out=o_t[:], in0=vps[:], scalar=bcol[:, 20 + j : 21 + j], in1=s_sb[:],
+                    op0=ALU.add, op1=ALU.mult,
+                )
+                oT[(j, c)] = o_t
+            if j < len(late):
+                prep(late[j])
+            if j > 0:
+                finish(j - 1)
+        finish(7)

@@ -15,30 +15,36 @@ ALU = mybir.AluOpType
 
 P = 128
 CH = 512
+BL = 256
+AHEAD = 4
 
 
 def tile_selectivemixing_pa_kernel(tc, x, W1, b1, W2g, b2g, Wv, bv, out):
     nc = tc.nc
     with ExitStack() as ctx:
+        ctx.enter_context(tc.manual_schedule())
         const = ctx.enter_context(tc.tile_pool(name="const", bufs=1))
         keep = ctx.enter_context(tc.tile_pool(name="keep", bufs=1))
-        stage = ctx.enter_context(tc.tile_pool(name="stage", bufs=6))
+        stage = ctx.enter_context(tc.tile_pool(name="stage", bufs=4))
+        wide = ctx.enter_context(tc.tile_pool(name="wide", bufs=2))
         tail = ctx.enter_context(tc.tile_pool(name="tail", bufs=3))
-        ps_acc = ctx.enter_context(tc.psum_pool(name="acc", bufs=4))
-        ps_tr = ctx.enter_context(tc.psum_pool(name="tr", bufs=4))
+        psum = ctx.enter_context(tc.psum_pool(name="psum", bufs=8))
 
-        ident_f = const.tile([P, P], F32, name="ident_f")
-        masks.make_identity(nc, ident_f[:])
-        ident_b = const.tile([P, P], BF16, name="ident_b")
-        masks.make_identity(nc, ident_b[:])
+        def bank(shape, dtype, name):
+            return psum.tile(shape, dtype, name=name, tag="bank")
+
         brow = const.tile([P, P], BF16, name="brow")
         nc.vector.memset(brow[:], 0.0)
         warm = const.tile([P, 4], F32, name="warm")
         nc.vector.memset(warm[:], 0.0)
-        nc.scalar.activation(out=warm[:, 1:2], in_=warm[:, 0:1], func=ACT.Silu)
         nc.scalar.dma_start(out=brow[0:12, :], in_=b1.rearrange("(j p) -> j p", p=P))
         nc.scalar.dma_start(out=brow[12:20, :], in_=b2g.rearrange("(j p) -> j p", p=P))
         nc.scalar.dma_start(out=brow[20:28, :], in_=bv.rearrange("(j p) -> j p", p=P))
+        nc.scalar.activation(out=warm[:, 1:2], in_=warm[:, 0:1], func=ACT.Silu)
+        ident_b = const.tile([P, P], BF16, name="ident_b")
+        masks.make_identity(nc, ident_b[:])
+        ident_f = const.tile([P, P], F32, name="ident_f")
+        masks.make_identity(nc, ident_f[:])
 
         xv = x.flatten_outer_dims().rearrange("(p i) k -> p i k", i=8)
         ov = out.flatten_outer_dims().rearrange("(p i) d -> p i d", i=8)
@@ -67,36 +73,36 @@ def tile_selectivemixing_pa_kernel(tc, x, W1, b1, W2g, b2g, Wv, bv, out):
             nc.sync.dma_start(out=t[:], in_=view[g, :, :, ch * CH : (ch + 1) * CH])
             raw[(nm, ch, g)] = t
 
-        load_x(0)
-        load_x(1)
         load_pairs(W1, "w1", 0, 0)
         load_pairs(W1, "w1", 0, 1)
-        load_x(2)
-        load_x(3)
+        load_x(0)
+        load_x(1)
         for ch in (1, 2):
             for g in range(2):
                 load_pairs(W1, "w1", ch, g)
+        load_x(2)
+        load_x(3)
         for ch in range(2):
             for g in range(2):
                 load_pairs(Wv, "wv", ch, g)
             for g in range(3):
                 load_rows(W2g, "w2", ch, g)
 
-        bt = ps_tr.tile([P, P], BF16, name="bt", tag="tr")
-        nc.tensor.transpose(bt[:], brow[:], ident_b[:])
-        bcol = const.tile([P, 32], F32, name="bcol")
-        nc.vector.tensor_copy(out=bcol[:, 0:28], in_=bt[:, 0:28])
-
         q = {}
 
-        def regroup(eng, src):
-            grp = stage.tile([P, CH, 4], BF16, name="grp", tag="grp", align_bytes=64)
-            o = grp[:].rearrange("p (c i) t -> p c t i", i=4)
-            s = src[:].rearrange("p t (c i) -> p c t i", i=4)
+        def copy_on(eng, o, s):
             if eng == "v":
                 nc.vector.tensor_copy(out=o, in_=s)
             else:
                 nc.scalar.copy(out=o, in_=s)
+
+        def regroup(eng, src):
+            grp = stage.tile([P, CH, 4], BF16, name="grp", tag="grp", align_bytes=64)
+            copy_on(
+                eng,
+                grp[:].rearrange("p (c i) t -> p c t i", i=4),
+                src[:].rearrange("p t (c i) -> p c t i", i=4),
+            )
             return grp
 
         def quantise(grp, key):
@@ -108,123 +114,195 @@ def tile_selectivemixing_pa_kernel(tc, x, W1, b1, W2g, b2g, Wv, bv, out):
                 scales=scales[:],
                 in_=grp[:].rearrange("p w j -> p (w j)"),
             )
-            q[key] = (codes, scales)
+            q[key] = (codes[:], scales[:])
 
-        def prep(jobs):
-            pending = None
-            for eng, src, key in jobs:
-                grp = regroup(eng, src)
-                if pending is not None:
-                    quantise(pending[0], pending[1])
-                pending = (grp, key)
-            quantise(pending[0], pending[1])
-
-        def mx(acc, wkey, col, xkey, start, stop):
-            wc, ws = q[wkey]
-            xc, xs = q[xkey]
+        def mx(acc, w, col, m, start, stop):
             nc.tensor.matmul_mx(
                 out=acc[:],
-                lhsT=wc[:, col * P : (col + 1) * P].bitcast(FP8X4),
-                lhsT_scale=ws[:, col * P : (col + 1) * P],
-                rhs=xc[:].bitcast(FP8X4),
-                rhs_scale=xs[:],
+                lhsT=w[0][:, col * P : (col + 1) * P].bitcast(FP8X4),
+                lhsT_scale=w[1][:, col * P : (col + 1) * P],
+                rhs=m[0].bitcast(FP8X4),
+                rhs_scale=m[1],
                 start=start,
                 stop=stop,
             )
 
-        def x_half(c):
-            grps = {}
-            for g in range(2):
-                grps[g] = stage.tile([P, CH, 4], BF16, name="gx", tag="grp", align_bytes=64)
+        def x_transposes(c):
+            banks = []
             for qq in range(2):
                 xw = x_sb[2 * c + qq][:].bitcast(F32)
                 for g in range(2):
-                    xt = ps_tr.tile([P, 2, 256], F32, name="xt", tag="tr")
+                    xt = bank([P, 2, 256], F32, "xt")
                     for u in range(2):
                         for ii in range(2):
                             lo = 256 * g + 128 * u
                             nc.tensor.transpose(
                                 xt[:, u, ii * P : (ii + 1) * P], xw[:, ii, lo : lo + P], ident_f[:]
                             )
-                    nc.scalar.copy(
-                        out=grps[g][:].bitcast(F32)[:, 256 * qq : 256 * qq + 256, :],
-                        in_=xt[:].rearrange("p u r -> p r u"),
-                    )
+                    banks.append((qq, g, xt))
+            return banks
+
+        def x_copies(banks):
+            grps = {}
+            for g in range(2):
+                grps[g] = stage.tile([P, CH, 4], BF16, name="gx", tag="grp", align_bytes=64)
+            for qq, g, xt in banks:
+                nc.scalar.copy(
+                    out=grps[g][:].bitcast(F32)[:, 256 * qq : 256 * qq + 256, :],
+                    in_=xt[:].rearrange("p u r -> p r u"),
+                )
             return grps
 
-        gx0 = x_half(0)
-        prep([("v", raw[("w1", 0, 0)], ("w1", 0, 0)), ("v", raw[("w1", 0, 1)], ("w1", 0, 1))])
-        quantise(gx0[0], ("x", 0, 0))
-        quantise(gx0[1], ("x", 1, 0))
-        gx1 = x_half(1)
-        prep([("v", raw[("w1", 1, 0)], ("w1", 1, 0)), ("v", raw[("w1", 1, 1)], ("w1", 1, 1))])
-        quantise(gx1[0], ("x", 0, 1))
-        quantise(gx1[1], ("x", 1, 1))
-        prep([("v", raw[("w1", 2, 0)], ("w1", 2, 0)), ("v", raw[("w1", 2, 1)], ("w1", 2, 1))])
-
         hT = {}
-        for fc in range(3):
-            for c in range(2):
-                hT[(fc, c)] = keep.tile([P, 4, CH], BF16, name="h_%d_%d" % (fc, c))
+
+        def layer1(fc, c):
+            hT[(fc, c)] = keep.tile([P, 4, CH], BF16, name="h_%d_%d" % (fc, c), tag="r_w1_%d_%d" % (fc, c))
             for jj in range(4):
-                for c in range(2):
-                    z = ps_acc.tile([P, CH], F32, name="z", tag="acc")
-                    for g in range(2):
-                        mx(z, ("w1", fc, g), jj, ("x", g, c), g == 0, g == 1)
-                    j = 4 * fc + jj
-                    nc.scalar.activation(
-                        out=hT[(fc, c)][:, jj, :], in_=z[:], func=ACT.Silu,
-                        bias=bcol[:, j : j + 1], scale=1.0,
-                    )
-            prep([("v", hT[(fc, 0)], ("h", fc, 0)), ("v", hT[(fc, 1)], ("h", fc, 1))])
-        nc.scalar.activation(out=warm[:, 2:3], in_=hT[(2, 1)][:, 3, 0:1], func=ACT.Sigmoid)
+                z = bank([P, CH], F32, "z")
+                for g in range(2):
+                    mx(z, q[("w1", fc, g)], jj, q[("x", g, c)], g == 0, g == 1)
+                j = 4 * fc + jj
+                nc.scalar.activation(
+                    out=hT[(fc, c)][:, jj, :], in_=z[:], func=ACT.Silu,
+                    bias=bcol[:, j : j + 1], scale=1.0,
+                )
 
-        prep([
-            ("s", raw[("wv", 0, 0)], ("wv", 0, 0)),
-            ("v", raw[("w2", 0, 0)], ("w2", 0, 0)),
-            ("s", raw[("wv", 0, 1)], ("wv", 0, 1)),
-            ("v", raw[("w2", 0, 1)], ("w2", 0, 1)),
-            ("v", raw[("w2", 0, 2)], ("w2", 0, 2)),
-        ])
-        late = [
-            [("v", raw[("w2", 1, 0)], ("w2", 1, 0)), ("v", raw[("w2", 1, 1)], ("w2", 1, 1))],
-            [("v", raw[("w2", 1, 2)], ("w2", 1, 2)), ("v", raw[("wv", 1, 0)], ("wv", 1, 0))],
-            [("v", raw[("wv", 1, 1)], ("wv", 1, 1))],
-        ]
+        blocks = {}
 
+        wgrp = {}
+
+        def block_part(b, eng, slices):
+            half, part = b // 2, b % 2
+            if b not in wgrp:
+                wgrp[b] = wide.tile([P, 5, BL, 4], BF16, name="wgrp", tag="wgrp", align_bytes=64)
+            srcs = [raw[("w2", half, g)] for g in range(3)] + [raw[("wv", half, g)] for g in range(2)]
+            for s in slices:
+                copy_on(
+                    eng,
+                    wgrp[b][:, s, :, :].rearrange("p (c i) t -> p c t i", i=4),
+                    srcs[s][:, :, part * BL : (part + 1) * BL].rearrange("p t (c i) -> p c t i", i=4),
+                )
+
+        def block_quantise(b):
+            grp = wgrp[b]
+            codes = keep.tile([P, 5, BL], U32, name="c_blk_%d" % b, align_bytes=64)
+            scales = keep.tile([P, 5, BL], U8, name="s_blk_%d" % b, align_bytes=64)
+            for lo, hi in ((0, 4), (4, 5)):
+                nc.vector.quantize_mx(
+                    out=codes[:, lo:hi, :].rearrange("p s w -> p (s w)").bitcast(FP8X4),
+                    scales=scales[:, lo:hi, :].rearrange("p s w -> p (s w)"),
+                    in_=grp[:, lo:hi, :, :].rearrange("p s w j -> p (s w j)"),
+                )
+            blocks[b] = (codes, scales)
+
+        def wslice(b, s):
+            return (blocks[b][0][:, s, :], blocks[b][1][:, s, :])
+
+        acc = {}
         oT = {}
 
-        def finish(j):
-            for c in range(2):
-                ot = ps_tr.tile([P, 4, P], F32, name="ot", tag="tr")
+        def open_unit(j, c):
+            b, col = j // 2, j % 2
+            vps = bank([P, CH], F32, "vps")
+            for g in range(2):
+                mx(vps, wslice(b, 3 + g), col, q[("x", g, c)], g == 0, g == 1)
+            gps = bank([P, CH], F32, "gps")
+            for g in range(2):
+                mx(gps, wslice(b, g), col, q[("h", g, c)], g == 0, False)
+            acc[(j, c)] = (gps, vps)
+
+        def close_unit(j, c):
+            b, col = j // 2, j % 2
+            gps, vps = acc[(j, c)]
+            mx(gps, wslice(b, 2), col, q[("h", 2, c)], False, True)
+            s_sb = tail.tile([P, CH], F32, name="s_sb", tag="s_sb")
+            nc.scalar.activation(
+                out=s_sb[:], in_=gps[:], func=ACT.Sigmoid,
+                bias=bcol[:, 12 + j : 13 + j], scale=1.0,
+            )
+            o_t = tail.tile([P, CH], F32, name="o_t", tag="o_t", bufs=6)
+            nc.vector.scalar_tensor_tensor(
+                out=o_t[:], in0=vps[:], scalar=bcol[:, 20 + j : 21 + j], in1=s_sb[:],
+                op0=ALU.add, op1=ALU.mult,
+            )
+            oT[(j, c)] = o_t
+
+        def finish(units):
+            ots = []
+            for j, c in units:
+                ot = bank([P, 4, P], F32, "ot")
                 for r in range(4):
                     nc.tensor.transpose(ot[:, r, :], oT[(j, c)][:, r * P : (r + 1) * P], ident_f[:])
+                ots.append(ot)
+            for (j, c), ot in zip(units, ots):
                 o_sb = tail.tile([P, 4, P], F32, name="o_sb", tag="o_sb")
                 nc.scalar.copy(out=o_sb[:], in_=ot[:])
                 nc.sync.dma_start(out=ov[:, 4 * c : 4 * c + 4, j * P : (j + 1) * P], in_=o_sb[:])
 
-        for j in range(8):
-            half, col = j // 4, j % 4
-            for c in range(2):
-                gps = ps_acc.tile([P, CH], F32, name="gps", tag="acc")
-                for g in range(3):
-                    mx(gps, ("w2", half, g), col, ("h", g, c), g == 0, g == 2)
-                vps = ps_acc.tile([P, CH], F32, name="vps", tag="acc")
-                for g in range(2):
-                    mx(vps, ("wv", half, g), col, ("x", g, c), g == 0, g == 1)
-                s_sb = tail.tile([P, CH], F32, name="s_sb", tag="s_sb")
-                nc.scalar.activation(
-                    out=s_sb[:], in_=gps[:], func=ACT.Sigmoid,
-                    bias=bcol[:, 12 + j : 13 + j], scale=1.0,
-                )
-                o_t = tail.tile([P, CH], F32, name="o_t", tag="o_t", bufs=4)
-                nc.vector.scalar_tensor_tensor(
-                    out=o_t[:], in0=vps[:], scalar=bcol[:, 20 + j : 21 + j], in1=s_sb[:],
-                    op0=ALU.add, op1=ALU.mult,
-                )
-                oT[(j, c)] = o_t
-            if j < len(late):
-                prep(late[j])
-            if j > 0:
-                finish(j - 1)
-        finish(7)
+        bt = bank([P, P], BF16, "bt")
+        nc.tensor.transpose(bt[:], brow[:], ident_b[:])
+        bcol = const.tile([P, 32], F32, name="bcol")
+        nc.vector.tensor_copy(out=bcol[:, 0:28], in_=bt[:, 0:28])
+
+        def h_prep(keys):
+            grps = [regroup("v", hT[k]) for k in keys]
+            for k, grp in zip(keys, grps):
+                quantise(grp, ("h", k[0], k[1]))
+
+        g00 = regroup("v", raw[("w1", 0, 0)])
+        g01 = regroup("s", raw[("w1", 0, 1)])
+        quantise(g00, ("w1", 0, 0))
+        quantise(g01, ("w1", 0, 1))
+        gx = x_copies(x_transposes(0))
+        g10 = regroup("s", raw[("w1", 1, 0)])
+        quantise(gx[0], ("x", 0, 0))
+        quantise(gx[1], ("x", 1, 0))
+        layer1(0, 0)
+        g11 = regroup("v", raw[("w1", 1, 1)])
+        quantise(g10, ("w1", 1, 0))
+        quantise(g11, ("w1", 1, 1))
+        layer1(1, 0)
+        g20 = regroup("v", raw[("w1", 2, 0)])
+        g21 = regroup("v", raw[("w1", 2, 1)])
+        quantise(g20, ("w1", 2, 0))
+        quantise(g21, ("w1", 2, 1))
+        xb = x_transposes(1)
+        gx = x_copies(xb)
+        layer1(2, 0)
+        h_prep([(0, 0)])
+        quantise(gx[0], ("x", 0, 1))
+        quantise(gx[1], ("x", 1, 1))
+        layer1(0, 1)
+        h_prep([(1, 0)])
+        block_part(0, "v", (3, 4))
+        layer1(1, 1)
+        h_prep([(2, 0)])
+        block_part(0, "v", (0, 1, 2))
+        block_quantise(0)
+        layer1(2, 1)
+        nc.scalar.activation(out=warm[:, 2:3], in_=hT[(2, 1)][:, 3, 0:1], func=ACT.Sigmoid)
+
+        units = [(2 * b + jj, c) for b in range(4) for c in range(2) for jj in range(2)]
+        for j, c in units[:2]:
+            open_unit(j, c)
+        h_prep([(0, 1), (1, 1)])
+        for j, c in units[2:4]:
+            open_unit(j, c)
+        block_part(1, "s", (3, 4))
+        h_prep([(2, 1)])
+        block_part(1, "v", (0, 1, 2))
+        block_quantise(1)
+
+        for n in range(16):
+            j, c = units[n]
+            if n >= AHEAD:
+                open_unit(j, c)
+            close_unit(j, c)
+            if n in (3, 7):
+                block_part(n // 4 + 2, "s", (3, 4))
+                block_part(n // 4 + 2, "v", (0, 1, 2))
+            if n in (4, 8):
+                block_quantise(n // 4 + 1)
+            if n % 2 == 1 and n >= 3:
+                finish(units[n - 3 : n - 1])
+        finish(units[14:16])

@@ -22,7 +22,6 @@ AHEAD = 4
 def tile_selectivemixing_pa_kernel(tc, x, W1, b1, W2g, b2g, Wv, bv, out):
     nc = tc.nc
     with ExitStack() as ctx:
-        ctx.enter_context(tc.manual_schedule())
         const = ctx.enter_context(tc.tile_pool(name="const", bufs=1))
         keep = ctx.enter_context(tc.tile_pool(name="keep", bufs=1))
         stage = ctx.enter_context(tc.tile_pool(name="stage", bufs=4))
@@ -227,17 +226,19 @@ def tile_selectivemixing_pa_kernel(tc, x, W1, b1, W2g, b2g, Wv, bv, out):
             )
             oT[(j, c)] = o_t
 
-        def finish(units):
+        def finish(pair):
             ots = []
-            for j, c in units:
+            for j, c in pair:
                 ot = bank([P, 4, P], F32, "ot")
                 for r in range(4):
                     nc.tensor.transpose(ot[:, r, :], oT[(j, c)][:, r * P : (r + 1) * P], ident_f[:])
                 ots.append(ot)
-            for (j, c), ot in zip(units, ots):
-                o_sb = tail.tile([P, 4, P], F32, name="o_sb", tag="o_sb")
-                nc.scalar.copy(out=o_sb[:], in_=ot[:])
-                nc.sync.dma_start(out=ov[:, 4 * c : 4 * c + 4, j * P : (j + 1) * P], in_=o_sb[:])
+            j0, c = pair[0]
+            o_sb = tail.tile([P, 4, 2 * P], F32, name="o_sb", tag="o_sb", bufs=4)
+            for k in range(2):
+                nc.scalar.copy(out=o_sb[:, :, k * P : (k + 1) * P], in_=ots[k][:])
+            nc.sync.dma_start(out=ov[:, 4 * c : 4 * c + 4, j0 * P : (j0 + 2) * P], in_=o_sb[:])
+
 
         bt = bank([P, P], BF16, "bt")
         nc.tensor.transpose(bt[:], brow[:], ident_b[:])

@@ -22,6 +22,7 @@ AHEAD = 4
 def tile_selectivemixing_pa_kernel(tc, x, W1, b1, W2g, b2g, Wv, bv, out):
     nc = tc.nc
     with ExitStack() as ctx:
+        ctx.enter_context(tc.manual_schedule())
         const = ctx.enter_context(tc.tile_pool(name="const", bufs=1))
         keep = ctx.enter_context(tc.tile_pool(name="keep", bufs=1))
         stage = ctx.enter_context(tc.tile_pool(name="stage", bufs=4))
@@ -198,6 +199,7 @@ def tile_selectivemixing_pa_kernel(tc, x, W1, b1, W2g, b2g, Wv, bv, out):
             return (blocks[b][0][:, s, :], blocks[b][1][:, s, :])
 
         acc = {}
+        sig = {}
         oT = {}
 
         def open_unit(j, c):
@@ -214,11 +216,16 @@ def tile_selectivemixing_pa_kernel(tc, x, W1, b1, W2g, b2g, Wv, bv, out):
             b, col = j // 2, j % 2
             gps, vps = acc[(j, c)]
             mx(gps, wslice(b, 2), col, q[("h", 2, c)], False, True)
-            s_sb = tail.tile([P, CH], F32, name="s_sb", tag="s_sb")
+            s_sb = tail.tile([P, CH], F32, name="s_sb", tag="s_sb", bufs=4)
             nc.scalar.activation(
                 out=s_sb[:], in_=gps[:], func=ACT.Sigmoid,
                 bias=bcol[:, 12 + j : 13 + j], scale=1.0,
             )
+            sig[(j, c)] = s_sb
+
+        def gate(j, c):
+            vps = acc[(j, c)][1]
+            s_sb = sig[(j, c)]
             o_t = tail.tile([P, CH], F32, name="o_t", tag="o_t", bufs=6)
             nc.vector.scalar_tensor_tensor(
                 out=o_t[:], in0=vps[:], scalar=bcol[:, 20 + j : 21 + j], in1=s_sb[:],
@@ -284,26 +291,30 @@ def tile_selectivemixing_pa_kernel(tc, x, W1, b1, W2g, b2g, Wv, bv, out):
         nc.scalar.activation(out=warm[:, 2:3], in_=hT[(2, 1)][:, 3, 0:1], func=ACT.Sigmoid)
 
         units = [(2 * b + jj, c) for b in range(4) for c in range(2) for jj in range(2)]
-        for j, c in units[:2]:
+        for j, c in units[0:2]:
             open_unit(j, c)
+            close_unit(j, c)
         h_prep([(0, 1), (1, 1)])
         for j, c in units[2:4]:
             open_unit(j, c)
+        for j, c in units[0:2]:
+            gate(j, c)
         block_part(1, "s", (3, 4))
         h_prep([(2, 1)])
+        finish(units[0:2])
         block_part(1, "v", (0, 1, 2))
         block_quantise(1)
 
-        for n in range(16):
+        for n in range(2, 16):
             j, c = units[n]
             if n >= AHEAD:
                 open_unit(j, c)
             close_unit(j, c)
+            gate(j, c)
             if n in (3, 7):
-                block_part(n // 4 + 2, "s", (3, 4))
-                block_part(n // 4 + 2, "v", (0, 1, 2))
+                block_part(n // 4 + 2, "v", (0, 1, 2, 3, 4))
             if n in (4, 8):
                 block_quantise(n // 4 + 1)
-            if n % 2 == 1 and n >= 3:
+            if n % 2 == 1 and n >= 5:
                 finish(units[n - 3 : n - 1])
         finish(units[14:16])

@@ -87,6 +87,9 @@ def tile_selectivemixing_pa_kernel(tc, x, W1, b1, W2g, b2g, Wv, bv, out):
                 load_pairs(Wv, "wv", ch, g)
             for g in range(3):
                 load_rows(W2g, "w2", ch, g)
+        bias_bc = const.tile([P, 2, BL], BF16, name="bias_bc")
+        nc.sync.dma_start(out=bias_bc[:, 0, :], in_=b2g[3 * BL : 4 * BL].partition_broadcast(P))
+        nc.sync.dma_start(out=bias_bc[:, 1, :], in_=bv[3 * BL : 4 * BL].partition_broadcast(P))
 
         q = {}
 
@@ -175,7 +178,7 @@ def tile_selectivemixing_pa_kernel(tc, x, W1, b1, W2g, b2g, Wv, bv, out):
             half, part = b // 2, b % 2
             if b not in wgrp:
                 wgrp[b] = wide.tile([P, 5, BL, 4], BF16, name="wgrp", tag="wgrp", align_bytes=64)
-            srcs = [raw[("w2", half, g)] for g in range(3)] + [raw[("wv", half, g)] for g in range(2)]
+            srcs = [raw[("wv", half, g)] for g in range(2)] + [raw[("w2", half, g)] for g in range(3)]
             for s in slices:
                 copy_on(
                     eng,
@@ -206,16 +209,16 @@ def tile_selectivemixing_pa_kernel(tc, x, W1, b1, W2g, b2g, Wv, bv, out):
             b, col = j // 2, j % 2
             vps = bank([P, CH], F32, "vps")
             for g in range(2):
-                mx(vps, wslice(b, 3 + g), col, q[("x", g, c)], g == 0, g == 1)
+                mx(vps, wslice(b, g), col, q[("x", g, c)], g == 0, g == 1)
             gps = bank([P, CH], F32, "gps")
             for g in range(2):
-                mx(gps, wslice(b, g), col, q[("h", g, c)], g == 0, False)
+                mx(gps, wslice(b, 2 + g), col, q[("h", g, c)], g == 0, False)
             acc[(j, c)] = (gps, vps)
 
         def close_unit(j, c):
             b, col = j // 2, j % 2
             gps, vps = acc[(j, c)]
-            mx(gps, wslice(b, 2), col, q[("h", 2, c)], False, True)
+            mx(gps, wslice(b, 4), col, q[("h", 2, c)], False, True)
             s_sb = tail.tile([P, CH], F32, name="s_sb", tag="s_sb", bufs=4)
             nc.scalar.activation(
                 out=s_sb[:], in_=gps[:], func=ACT.Sigmoid,
@@ -233,7 +236,7 @@ def tile_selectivemixing_pa_kernel(tc, x, W1, b1, W2g, b2g, Wv, bv, out):
             )
             oT[(j, c)] = o_t
 
-        def finish(pair):
+        def finish(pair, engines="ss"):
             ots = []
             for j, c in pair:
                 ot = bank([P, 4, P], F32, "ot")
@@ -243,22 +246,52 @@ def tile_selectivemixing_pa_kernel(tc, x, W1, b1, W2g, b2g, Wv, bv, out):
             j0, c = pair[0]
             o_sb = tail.tile([P, 4, 2 * P], F32, name="o_sb", tag="o_sb", bufs=4)
             for k in range(2):
-                nc.scalar.copy(out=o_sb[:, :, k * P : (k + 1) * P], in_=ots[k][:])
+                copy_on(engines[k], o_sb[:, :, k * P : (k + 1) * P], ots[k][:])
             nc.sync.dma_start(out=ov[:, 4 * c : 4 * c + 4, j0 * P : (j0 + 2) * P], in_=o_sb[:])
 
+
+        def direct_group(b, c):
+            waiting = []
+            for r in range(4):
+                gv = bank([P, 2, BL], F32, "gv")
+                for g in range(3):
+                    nc.tensor.matmul_mx(
+                        out=gv[:, 0, :],
+                        lhsT=q[("h", g, c)][0][:, r * P : (r + 1) * P].bitcast(FP8X4),
+                        lhsT_scale=q[("h", g, c)][1][:, r * P : (r + 1) * P],
+                        rhs=wslice(b, 2 + g)[0].bitcast(FP8X4), rhs_scale=wslice(b, 2 + g)[1],
+                        start=g == 0, stop=g == 2,
+                    )
+                for g in range(2):
+                    nc.tensor.matmul_mx(
+                        out=gv[:, 1, :],
+                        lhsT=q[("x", g, c)][0][:, r * P : (r + 1) * P].bitcast(FP8X4),
+                        lhsT_scale=q[("x", g, c)][1][:, r * P : (r + 1) * P],
+                        rhs=wslice(b, g)[0].bitcast(FP8X4), rhs_scale=wslice(b, g)[1],
+                        start=g == 0, stop=g == 1,
+                    )
+                a_sb = tail.tile([P, 2, BL], F32, name="a_sb", tag="o_t", bufs=6)
+                nc.vector.tensor_tensor(out=a_sb[:], in0=gv[:], in1=bias_bc[:], op=ALU.add)
+                s_d = tail.tile([P, BL], F32, name="s_d", tag="s_sb", bufs=4)
+                nc.scalar.activation(out=s_d[:], in_=a_sb[:, 0, :], func=ACT.Sigmoid)
+                waiting.append((r, a_sb, s_d))
+                if len(waiting) > 1:
+                    multiply(b, c, waiting.pop(0))
+            multiply(b, c, waiting.pop(0))
+
+        def multiply(b, c, item):
+            r, a_sb, s_d = item
+            o_d = tail.tile([P, BL], F32, name="o_d", tag="o_d", bufs=4)
+            nc.vector.tensor_tensor(out=o_d[:], in0=a_sb[:, 1, :], in1=s_d[:], op=ALU.mult)
+            nc.sync.dma_start(out=ov[:, 4 * c + r, b * BL : (b + 1) * BL], in_=o_d[:])
 
         bt = bank([P, P], BF16, "bt")
         nc.tensor.transpose(bt[:], brow[:], ident_b[:])
         bcol = const.tile([P, 32], F32, name="bcol")
         nc.vector.tensor_copy(out=bcol[:, 0:28], in_=bt[:, 0:28])
 
-        def h_prep(keys):
-            grps = [regroup("v", hT[k]) for k in keys]
-            for k, grp in zip(keys, grps):
-                quantise(grp, ("h", k[0], k[1]))
-
         g00 = regroup("v", raw[("w1", 0, 0)])
-        g01 = regroup("s", raw[("w1", 0, 1)])
+        g01 = regroup("v", raw[("w1", 0, 1)])
         quantise(g00, ("w1", 0, 0))
         quantise(g01, ("w1", 0, 1))
         gx = x_copies(x_transposes(0))
@@ -274,18 +307,22 @@ def tile_selectivemixing_pa_kernel(tc, x, W1, b1, W2g, b2g, Wv, bv, out):
         g21 = regroup("v", raw[("w1", 2, 1)])
         quantise(g20, ("w1", 2, 0))
         quantise(g21, ("w1", 2, 1))
-        xb = x_transposes(1)
-        gx = x_copies(xb)
+        gx = x_copies(x_transposes(1))
         layer1(2, 0)
-        h_prep([(0, 0)])
+        h00 = regroup("v", hT[(0, 0)])
         quantise(gx[0], ("x", 0, 1))
+        quantise(h00, ("h", 0, 0))
         quantise(gx[1], ("x", 1, 1))
         layer1(0, 1)
-        h_prep([(1, 0)])
-        block_part(0, "v", (3, 4))
+        h10 = regroup("v", hT[(1, 0)])
+        block_part(0, "v", (0,))
+        quantise(h10, ("h", 1, 0))
+        block_part(0, "v", (1,))
         layer1(1, 1)
-        h_prep([(2, 0)])
-        block_part(0, "v", (0, 1, 2))
+        h20 = regroup("v", hT[(2, 0)])
+        block_part(0, "v", (2,))
+        quantise(h20, ("h", 2, 0))
+        block_part(0, "v", (3, 4))
         block_quantise(0)
         layer1(2, 1)
         nc.scalar.activation(out=warm[:, 2:3], in_=hT[(2, 1)][:, 3, 0:1], func=ACT.Sigmoid)
@@ -294,18 +331,23 @@ def tile_selectivemixing_pa_kernel(tc, x, W1, b1, W2g, b2g, Wv, bv, out):
         for j, c in units[0:2]:
             open_unit(j, c)
             close_unit(j, c)
-        h_prep([(0, 1), (1, 1)])
+        h01 = regroup("v", hT[(0, 1)])
+        h11 = regroup("v", hT[(1, 1)])
+        quantise(h01, ("h", 0, 1))
+        quantise(h11, ("h", 1, 1))
         for j, c in units[2:4]:
             open_unit(j, c)
         for j, c in units[0:2]:
             gate(j, c)
-        block_part(1, "s", (3, 4))
-        h_prep([(2, 1)])
+        block_part(1, "s", (0, 1))
+        h21 = regroup("v", hT[(2, 1)])
+        block_part(1, "v", (2,))
+        quantise(h21, ("h", 2, 1))
         finish(units[0:2])
-        block_part(1, "v", (0, 1, 2))
+        block_part(1, "v", (3, 4))
         block_quantise(1)
 
-        for n in range(2, 16):
+        for n in range(2, 12):
             j, c = units[n]
             if n >= AHEAD:
                 open_unit(j, c)
@@ -317,4 +359,6 @@ def tile_selectivemixing_pa_kernel(tc, x, W1, b1, W2g, b2g, Wv, bv, out):
                 block_quantise(n // 4 + 1)
             if n % 2 == 1 and n >= 5:
                 finish(units[n - 3 : n - 1])
-        finish(units[14:16])
+        direct_group(3, 0)
+        finish(units[10:12])
+        direct_group(3, 1)

@@ -14,9 +14,12 @@ ACT = mybir.ActivationFunctionType
 ALU = mybir.AluOpType
 
 P = 128
-CH = 512
-BL = 256
-AHEAD = 4
+PACK = 4
+CHUNK = 512
+BLOCK = 256
+SLICES = 5
+DIRECT = 3
+B1_AT, B2G_AT, BV_AT, BIAS_TILES = 0, 12, 20, 28
 
 
 def tile_selectivemixing_pa_kernel(tc, x, W1, b1, W2g, b2g, Wv, bv, out):
@@ -27,338 +30,333 @@ def tile_selectivemixing_pa_kernel(tc, x, W1, b1, W2g, b2g, Wv, bv, out):
         keep = ctx.enter_context(tc.tile_pool(name="keep", bufs=1))
         stage = ctx.enter_context(tc.tile_pool(name="stage", bufs=4))
         wide = ctx.enter_context(tc.tile_pool(name="wide", bufs=2))
-        tail = ctx.enter_context(tc.tile_pool(name="tail", bufs=3))
+        tail = ctx.enter_context(tc.tile_pool(name="tail", bufs=4))
         psum = ctx.enter_context(tc.psum_pool(name="psum", bufs=8))
 
         def bank(shape, dtype, name):
             return psum.tile(shape, dtype, name=name, tag="bank")
 
-        brow = const.tile([P, P], BF16, name="brow")
-        nc.vector.memset(brow[:], 0.0)
+        bias_rows = const.tile([P, P], BF16, name="bias_rows")
+        nc.vector.memset(bias_rows[:], 0.0)
         warm = const.tile([P, 4], F32, name="warm")
         nc.vector.memset(warm[:], 0.0)
-        nc.scalar.dma_start(out=brow[0:12, :], in_=b1.rearrange("(j p) -> j p", p=P))
-        nc.scalar.dma_start(out=brow[12:20, :], in_=b2g.rearrange("(j p) -> j p", p=P))
-        nc.scalar.dma_start(out=brow[20:28, :], in_=bv.rearrange("(j p) -> j p", p=P))
+        for vec, at, end in ((b1, B1_AT, B2G_AT), (b2g, B2G_AT, BV_AT), (bv, BV_AT, BIAS_TILES)):
+            nc.scalar.dma_start(out=bias_rows[at:end, :], in_=vec.rearrange("(j p) -> j p", p=P))
         nc.scalar.activation(out=warm[:, 1:2], in_=warm[:, 0:1], func=ACT.Silu)
-        ident_b = const.tile([P, P], BF16, name="ident_b")
-        masks.make_identity(nc, ident_b[:])
-        ident_f = const.tile([P, P], F32, name="ident_f")
-        masks.make_identity(nc, ident_f[:])
+        ident_bf16 = const.tile([P, P], BF16, name="ident_bf16")
+        masks.make_identity(nc, ident_bf16[:])
+        ident_f32 = const.tile([P, P], F32, name="ident_f32")
+        masks.make_identity(nc, ident_f32[:])
 
-        xv = x.flatten_outer_dims().rearrange("(p i) k -> p i k", i=8)
-        ov = out.flatten_outer_dims().rearrange("(p i) d -> p i d", i=8)
-        x_sb = {}
-        raw = {}
+        x_view = x.flatten_outer_dims().rearrange("(p i) k -> p i k", i=8)
+        out_view = out.flatten_outer_dims().rearrange("(p i) d -> p i d", i=8)
+        x_tiles = {}
+        rows = {}
 
-        def load_x(q):
-            t = keep.tile([P, 2, 1024], BF16, name="x_%d" % q)
-            nc.sync.dma_start(out=t[:], in_=xv[:, 2 * q : 2 * q + 2, :])
-            x_sb[q] = t
+        def load_x(pair):
+            t = keep.tile([P, 2, 1024], BF16, name="x_%d" % pair)
+            nc.sync.dma_start(out=t[:], in_=x_view[:, 2 * pair : 2 * pair + 2, :])
+            x_tiles[pair] = t
 
-        def load_pairs(W, nm, ch, g):
+        def load_k_pairs(W, name, chunk, g):
             view = W.rearrange("(a p e) f -> e p a f", a=4, p=P, e=2)
-            t = keep.tile([P, 4, CH], BF16, name="r_%s_%d_%d" % (nm, ch, g))
-            tv = t[:].rearrange("p (u e) f -> p u e f", e=2)
+            t = keep.tile([P, PACK, CHUNK], BF16, name="rows_%s_%d_%d" % (name, chunk, g))
+            by_e = t[:].rearrange("p (u e) f -> p u e f", e=2)
             for e in range(2):
                 nc.sync.dma_start(
-                    out=tv[:, :, e, :],
-                    in_=view[e, :, 2 * g : 2 * g + 2, ch * CH : (ch + 1) * CH],
+                    out=by_e[:, :, e, :],
+                    in_=view[e, :, 2 * g : 2 * g + 2, chunk * CHUNK : (chunk + 1) * CHUNK],
                 )
-            raw[(nm, ch, g)] = t
+            rows[(name, chunk, g)] = t
 
-        def load_rows(W, nm, ch, g):
-            view = W.rearrange("(g t p) n -> g p t n", g=3, t=4, p=P)
-            t = keep.tile([P, 4, CH], BF16, name="r_%s_%d_%d" % (nm, ch, g))
-            nc.sync.dma_start(out=t[:], in_=view[g, :, :, ch * CH : (ch + 1) * CH])
-            raw[(nm, ch, g)] = t
+        def load_k_rows(W, name, chunk, g):
+            view = W.rearrange("(g t p) n -> g p t n", g=3, t=PACK, p=P)
+            t = keep.tile([P, PACK, CHUNK], BF16, name="rows_%s_%d_%d" % (name, chunk, g))
+            nc.sync.dma_start(out=t[:], in_=view[g, :, :, chunk * CHUNK : (chunk + 1) * CHUNK])
+            rows[(name, chunk, g)] = t
 
-        load_pairs(W1, "w1", 0, 0)
-        load_pairs(W1, "w1", 0, 1)
-        load_x(0)
-        load_x(1)
-        for ch in (1, 2):
+        for g in range(2):
+            load_k_pairs(W1, "w1", 0, g)
+        for pair in (0, 1):
+            load_x(pair)
+        for chunk in (1, 2):
             for g in range(2):
-                load_pairs(W1, "w1", ch, g)
-        load_x(2)
-        load_x(3)
-        for ch in range(2):
+                load_k_pairs(W1, "w1", chunk, g)
+        for pair in (2, 3):
+            load_x(pair)
+        for chunk in range(2):
             for g in range(2):
-                load_pairs(Wv, "wv", ch, g)
+                load_k_pairs(Wv, "wv", chunk, g)
             for g in range(3):
-                load_rows(W2g, "w2", ch, g)
-        bias_bc = const.tile([P, 2, BL], BF16, name="bias_bc")
-        nc.sync.dma_start(out=bias_bc[:, 0, :], in_=b2g[3 * BL : 4 * BL].partition_broadcast(P))
-        nc.sync.dma_start(out=bias_bc[:, 1, :], in_=bv[3 * BL : 4 * BL].partition_broadcast(P))
+                load_k_rows(W2g, "w2", chunk, g)
+        bias_free = const.tile([P, 2, BLOCK], BF16, name="bias_free")
+        direct_cols = slice(DIRECT * BLOCK, (DIRECT + 1) * BLOCK)
+        nc.sync.dma_start(out=bias_free[:, 0, :], in_=b2g[direct_cols].partition_broadcast(P))
+        nc.sync.dma_start(out=bias_free[:, 1, :], in_=bv[direct_cols].partition_broadcast(P))
 
-        q = {}
+        mx = {}
 
-        def copy_on(eng, o, s):
-            if eng == "v":
-                nc.vector.tensor_copy(out=o, in_=s)
+        def copy_on(engine, dst, src):
+            if engine == "vector":
+                nc.vector.tensor_copy(out=dst, in_=src)
             else:
-                nc.scalar.copy(out=o, in_=s)
+                nc.scalar.copy(out=dst, in_=src)
 
-        def regroup(eng, src):
-            grp = stage.tile([P, CH, 4], BF16, name="grp", tag="grp", align_bytes=64)
+        def side_by_side(engine, dst, src):
             copy_on(
-                eng,
-                grp[:].rearrange("p (c i) t -> p c t i", i=4),
-                src[:].rearrange("p t (c i) -> p c t i", i=4),
+                engine,
+                dst.rearrange("p (c i) t -> p c t i", i=4),
+                src.rearrange("p t (c i) -> p c t i", i=4),
             )
-            return grp
 
-        def quantise(grp, key):
-            nm = "%s_%d_%d" % key
-            codes = keep.tile([P, CH], U32, name="c_" + nm, align_bytes=64)
-            scales = keep.tile([P, CH], U8, name="s_" + nm, align_bytes=64)
+        def regroup(engine, src):
+            grouped = stage.tile([P, CHUNK, PACK], BF16, name="grouped", tag="grouped", align_bytes=64)
+            side_by_side(engine, grouped[:], src[:])
+            return grouped
+
+        def quantise(grouped, key):
+            name = "%s_%d_%d" % key
+            words = keep.tile([P, CHUNK], U32, name="words_" + name, align_bytes=64)
+            scales = keep.tile([P, CHUNK], U8, name="scales_" + name, align_bytes=64)
             nc.vector.quantize_mx(
-                out=codes[:].bitcast(FP8X4),
+                out=words[:].bitcast(FP8X4),
                 scales=scales[:],
-                in_=grp[:].rearrange("p w j -> p (w j)"),
+                in_=grouped[:].rearrange("p w t -> p (w t)"),
             )
-            q[key] = (codes[:], scales[:])
+            mx[key] = (words[:], scales[:])
 
-        def mx(acc, w, col, m, start, stop):
+        def mx_pass(acc, stationary, tile_index, moving, start, stop):
+            cols = slice(tile_index * P, (tile_index + 1) * P)
             nc.tensor.matmul_mx(
-                out=acc[:],
-                lhsT=w[0][:, col * P : (col + 1) * P].bitcast(FP8X4),
-                lhsT_scale=w[1][:, col * P : (col + 1) * P],
-                rhs=m[0].bitcast(FP8X4),
-                rhs_scale=m[1],
+                out=acc,
+                lhsT=stationary[0][:, cols].bitcast(FP8X4),
+                lhsT_scale=stationary[1][:, cols],
+                rhs=moving[0].bitcast(FP8X4),
+                rhs_scale=moving[1],
                 start=start,
                 stop=stop,
             )
 
-        def x_transposes(c):
+        def transpose_x(c):
             banks = []
-            for qq in range(2):
-                xw = x_sb[2 * c + qq][:].bitcast(F32)
+            for pair in range(2):
+                x_words = x_tiles[2 * c + pair][:].bitcast(F32)
                 for g in range(2):
-                    xt = bank([P, 2, 256], F32, "xt")
+                    xt = bank([P, 2, 2 * P], F32, "xt")
                     for u in range(2):
-                        for ii in range(2):
-                            lo = 256 * g + 128 * u
+                        for i in range(2):
+                            first = 256 * g + 128 * u
                             nc.tensor.transpose(
-                                xt[:, u, ii * P : (ii + 1) * P], xw[:, ii, lo : lo + P], ident_f[:]
+                                xt[:, u, i * P : (i + 1) * P],
+                                x_words[:, i, first : first + P],
+                                ident_f32[:],
                             )
-                    banks.append((qq, g, xt))
+                    banks.append((pair, g, xt))
             return banks
 
-        def x_copies(banks):
-            grps = {}
+        def copy_x(banks):
+            grouped = {}
             for g in range(2):
-                grps[g] = stage.tile([P, CH, 4], BF16, name="gx", tag="grp", align_bytes=64)
-            for qq, g, xt in banks:
+                grouped[g] = stage.tile(
+                    [P, CHUNK, PACK], BF16, name="grouped_x", tag="grouped", align_bytes=64
+                )
+            for pair, g, xt in banks:
                 nc.scalar.copy(
-                    out=grps[g][:].bitcast(F32)[:, 256 * qq : 256 * qq + 256, :],
+                    out=grouped[g][:].bitcast(F32)[:, 2 * P * pair : 2 * P * (pair + 1), :],
                     in_=xt[:].rearrange("p u r -> p r u"),
                 )
-            return grps
+            return grouped
 
-        hT = {}
+        h_rows = {}
 
-        def layer1(fc, c):
-            hT[(fc, c)] = keep.tile([P, 4, CH], BF16, name="h_%d_%d" % (fc, c), tag="r_w1_%d_%d" % (fc, c))
-            for jj in range(4):
-                z = bank([P, CH], F32, "z")
+        def first_layer(g2, c):
+            h_rows[(g2, c)] = keep.tile(
+                [P, PACK, CHUNK], BF16, name="h_%d_%d" % (g2, c), tag="rows_w1_%d_%d" % (g2, c)
+            )
+            for t in range(PACK):
+                z = bank([P, CHUNK], F32, "z")
                 for g in range(2):
-                    mx(z, q[("w1", fc, g)], jj, q[("x", g, c)], g == 0, g == 1)
-                j = 4 * fc + jj
+                    mx_pass(z[:], mx[("w1", g2, g)], t, mx[("x", g, c)], g == 0, g == 1)
+                at = B1_AT + PACK * g2 + t
                 nc.scalar.activation(
-                    out=hT[(fc, c)][:, jj, :], in_=z[:], func=ACT.Silu,
-                    bias=bcol[:, j : j + 1], scale=1.0,
+                    out=h_rows[(g2, c)][:, t, :], in_=z[:], func=ACT.Silu,
+                    bias=bias_cols[:, at : at + 1], scale=1.0,
                 )
 
-        blocks = {}
+        block_grouped = {}
+        block_mx = {}
 
-        wgrp = {}
-
-        def block_part(b, eng, slices):
-            half, part = b // 2, b % 2
-            if b not in wgrp:
-                wgrp[b] = wide.tile([P, 5, BL, 4], BF16, name="wgrp", tag="wgrp", align_bytes=64)
-            srcs = [raw[("wv", half, g)] for g in range(2)] + [raw[("w2", half, g)] for g in range(3)]
+        def regroup_block(b, engine, slices):
+            chunk, part = b // 2, b % 2
+            if b not in block_grouped:
+                block_grouped[b] = wide.tile(
+                    [P, SLICES, BLOCK, PACK], BF16, name="block_grouped", tag="block_grouped", align_bytes=64
+                )
+            sources = [rows[("wv", chunk, g)] for g in range(2)] + [rows[("w2", chunk, g)] for g in range(3)]
             for s in slices:
-                copy_on(
-                    eng,
-                    wgrp[b][:, s, :, :].rearrange("p (c i) t -> p c t i", i=4),
-                    srcs[s][:, :, part * BL : (part + 1) * BL].rearrange("p t (c i) -> p c t i", i=4),
+                side_by_side(
+                    engine,
+                    block_grouped[b][:, s, :, :],
+                    sources[s][:, :, part * BLOCK : (part + 1) * BLOCK],
                 )
 
-        def block_quantise(b):
-            grp = wgrp[b]
-            codes = keep.tile([P, 5, BL], U32, name="c_blk_%d" % b, align_bytes=64)
-            scales = keep.tile([P, 5, BL], U8, name="s_blk_%d" % b, align_bytes=64)
+        def quantise_block(b):
+            grouped = block_grouped[b]
+            words = keep.tile([P, SLICES, BLOCK], U32, name="words_block_%d" % b, align_bytes=64)
+            scales = keep.tile([P, SLICES, BLOCK], U8, name="scales_block_%d" % b, align_bytes=64)
             for lo, hi in ((0, 4), (4, 5)):
                 nc.vector.quantize_mx(
-                    out=codes[:, lo:hi, :].rearrange("p s w -> p (s w)").bitcast(FP8X4),
+                    out=words[:, lo:hi, :].rearrange("p s w -> p (s w)").bitcast(FP8X4),
                     scales=scales[:, lo:hi, :].rearrange("p s w -> p (s w)"),
-                    in_=grp[:, lo:hi, :, :].rearrange("p s w j -> p (s w j)"),
+                    in_=grouped[:, lo:hi, :, :].rearrange("p s w t -> p (s w t)"),
                 )
-            blocks[b] = (codes, scales)
+            block_mx[b] = (words, scales)
 
-        def wslice(b, s):
-            return (blocks[b][0][:, s, :], blocks[b][1][:, s, :])
+        def wv_slice(b, g):
+            return (block_mx[b][0][:, g, :], block_mx[b][1][:, g, :])
 
-        acc = {}
-        sig = {}
-        oT = {}
+        def w2_slice(b, g):
+            return (block_mx[b][0][:, 2 + g, :], block_mx[b][1][:, 2 + g, :])
+
+        sums = {}
+        gates = {}
+        products = {}
 
         def open_unit(j, c):
-            b, col = j // 2, j % 2
-            vps = bank([P, CH], F32, "vps")
+            b, tile_index = j // 2, j % 2
+            v = bank([P, CHUNK], F32, "v")
             for g in range(2):
-                mx(vps, wslice(b, g), col, q[("x", g, c)], g == 0, g == 1)
-            gps = bank([P, CH], F32, "gps")
+                mx_pass(v[:], wv_slice(b, g), tile_index, mx[("x", g, c)], g == 0, g == 1)
+            gsum = bank([P, CHUNK], F32, "gsum")
             for g in range(2):
-                mx(gps, wslice(b, 2 + g), col, q[("h", g, c)], g == 0, False)
-            acc[(j, c)] = (gps, vps)
+                mx_pass(gsum[:], w2_slice(b, g), tile_index, mx[("h", g, c)], g == 0, False)
+            sums[(j, c)] = (gsum, v)
 
         def close_unit(j, c):
-            b, col = j // 2, j % 2
-            gps, vps = acc[(j, c)]
-            mx(gps, wslice(b, 4), col, q[("h", 2, c)], False, True)
-            s_sb = tail.tile([P, CH], F32, name="s_sb", tag="s_sb", bufs=4)
+            gsum = sums[(j, c)][0]
+            mx_pass(gsum[:], w2_slice(j // 2, 2), j % 2, mx[("h", 2, c)], False, True)
+            s = tail.tile([P, CHUNK], F32, name="gate", tag="gate")
             nc.scalar.activation(
-                out=s_sb[:], in_=gps[:], func=ACT.Sigmoid,
-                bias=bcol[:, 12 + j : 13 + j], scale=1.0,
+                out=s[:], in_=gsum[:], func=ACT.Sigmoid,
+                bias=bias_cols[:, B2G_AT + j : B2G_AT + j + 1], scale=1.0,
             )
-            sig[(j, c)] = s_sb
+            gates[(j, c)] = s
 
-        def gate(j, c):
-            vps = acc[(j, c)][1]
-            s_sb = sig[(j, c)]
-            o_t = tail.tile([P, CH], F32, name="o_t", tag="o_t", bufs=6)
+        def multiply_unit(j, c):
+            prod = tail.tile([P, CHUNK], F32, name="product", tag="product", bufs=6)
             nc.vector.scalar_tensor_tensor(
-                out=o_t[:], in0=vps[:], scalar=bcol[:, 20 + j : 21 + j], in1=s_sb[:],
-                op0=ALU.add, op1=ALU.mult,
+                out=prod[:], in0=sums[(j, c)][1][:], scalar=bias_cols[:, BV_AT + j : BV_AT + j + 1],
+                in1=gates[(j, c)][:], op0=ALU.add, op1=ALU.mult,
             )
-            oT[(j, c)] = o_t
+            products[(j, c)] = prod
 
-        def finish(pair, engines="ss"):
-            ots = []
-            for j, c in pair:
-                ot = bank([P, 4, P], F32, "ot")
+        def store_pair(pair):
+            banks = []
+            for unit in pair:
+                back = bank([P, 4, P], F32, "back")
                 for r in range(4):
-                    nc.tensor.transpose(ot[:, r, :], oT[(j, c)][:, r * P : (r + 1) * P], ident_f[:])
-                ots.append(ot)
-            j0, c = pair[0]
-            o_sb = tail.tile([P, 4, 2 * P], F32, name="o_sb", tag="o_sb", bufs=4)
+                    nc.tensor.transpose(back[:, r, :], products[unit][:, r * P : (r + 1) * P], ident_f32[:])
+                banks.append(back)
+            j, c = pair[0]
+            result = tail.tile([P, 4, 2 * P], F32, name="result", tag="result")
             for k in range(2):
-                copy_on(engines[k], o_sb[:, :, k * P : (k + 1) * P], ots[k][:])
-            nc.sync.dma_start(out=ov[:, 4 * c : 4 * c + 4, j0 * P : (j0 + 2) * P], in_=o_sb[:])
+                nc.scalar.copy(out=result[:, :, k * P : (k + 1) * P], in_=banks[k][:])
+            nc.sync.dma_start(out=out_view[:, 4 * c : 4 * c + 4, j * P : (j + 2) * P], in_=result[:])
 
+        def direct_multiply(c, r, biased, s):
+            result = tail.tile([P, BLOCK], F32, name="direct_result", tag="direct_result")
+            nc.vector.tensor_tensor(out=result[:], in0=biased[:, 1, :], in1=s[:], op=ALU.mult)
+            nc.sync.dma_start(out=out_view[:, 4 * c + r, direct_cols], in_=result[:])
 
-        def direct_group(b, c):
+        def direct_half(c):
             waiting = []
             for r in range(4):
-                gv = bank([P, 2, BL], F32, "gv")
+                gv = bank([P, 2, BLOCK], F32, "gv")
                 for g in range(3):
-                    nc.tensor.matmul_mx(
-                        out=gv[:, 0, :],
-                        lhsT=q[("h", g, c)][0][:, r * P : (r + 1) * P].bitcast(FP8X4),
-                        lhsT_scale=q[("h", g, c)][1][:, r * P : (r + 1) * P],
-                        rhs=wslice(b, 2 + g)[0].bitcast(FP8X4), rhs_scale=wslice(b, 2 + g)[1],
-                        start=g == 0, stop=g == 2,
-                    )
+                    mx_pass(gv[:, 0, :], mx[("h", g, c)], r, w2_slice(DIRECT, g), g == 0, g == 2)
                 for g in range(2):
-                    nc.tensor.matmul_mx(
-                        out=gv[:, 1, :],
-                        lhsT=q[("x", g, c)][0][:, r * P : (r + 1) * P].bitcast(FP8X4),
-                        lhsT_scale=q[("x", g, c)][1][:, r * P : (r + 1) * P],
-                        rhs=wslice(b, g)[0].bitcast(FP8X4), rhs_scale=wslice(b, g)[1],
-                        start=g == 0, stop=g == 1,
-                    )
-                a_sb = tail.tile([P, 2, BL], F32, name="a_sb", tag="o_t", bufs=6)
-                nc.vector.tensor_tensor(out=a_sb[:], in0=gv[:], in1=bias_bc[:], op=ALU.add)
-                s_d = tail.tile([P, BL], F32, name="s_d", tag="s_sb", bufs=4)
-                nc.scalar.activation(out=s_d[:], in_=a_sb[:, 0, :], func=ACT.Sigmoid)
-                waiting.append((r, a_sb, s_d))
+                    mx_pass(gv[:, 1, :], mx[("x", g, c)], r, wv_slice(DIRECT, g), g == 0, g == 1)
+                biased = tail.tile([P, 2, BLOCK], F32, name="biased", tag="product", bufs=6)
+                nc.vector.tensor_tensor(out=biased[:], in0=gv[:], in1=bias_free[:], op=ALU.add)
+                s = tail.tile([P, BLOCK], F32, name="direct_gate", tag="gate")
+                nc.scalar.activation(out=s[:], in_=biased[:, 0, :], func=ACT.Sigmoid)
+                waiting.append((r, biased, s))
                 if len(waiting) > 1:
-                    multiply(b, c, waiting.pop(0))
-            multiply(b, c, waiting.pop(0))
+                    direct_multiply(c, *waiting.pop(0))
+            direct_multiply(c, *waiting.pop(0))
 
-        def multiply(b, c, item):
-            r, a_sb, s_d = item
-            o_d = tail.tile([P, BL], F32, name="o_d", tag="o_d", bufs=4)
-            nc.vector.tensor_tensor(out=o_d[:], in0=a_sb[:, 1, :], in1=s_d[:], op=ALU.mult)
-            nc.sync.dma_start(out=ov[:, 4 * c + r, b * BL : (b + 1) * BL], in_=o_d[:])
+        bias_t = bank([P, P], BF16, "bias_t")
+        nc.tensor.transpose(bias_t[:], bias_rows[:], ident_bf16[:])
+        bias_cols = const.tile([P, 32], F32, name="bias_cols")
+        nc.vector.tensor_copy(out=bias_cols[:, 0:BIAS_TILES], in_=bias_t[:, 0:BIAS_TILES])
 
-        bt = bank([P, P], BF16, "bt")
-        nc.tensor.transpose(bt[:], brow[:], ident_b[:])
-        bcol = const.tile([P, 32], F32, name="bcol")
-        nc.vector.tensor_copy(out=bcol[:, 0:28], in_=bt[:, 0:28])
+        w1_00 = regroup("vector", rows[("w1", 0, 0)])
+        w1_01 = regroup("vector", rows[("w1", 0, 1)])
+        quantise(w1_00, ("w1", 0, 0))
+        quantise(w1_01, ("w1", 0, 1))
+        x_grouped = copy_x(transpose_x(0))
+        w1_10 = regroup("scalar", rows[("w1", 1, 0)])
+        quantise(x_grouped[0], ("x", 0, 0))
+        quantise(x_grouped[1], ("x", 1, 0))
+        first_layer(0, 0)
+        w1_11 = regroup("vector", rows[("w1", 1, 1)])
+        quantise(w1_10, ("w1", 1, 0))
+        quantise(w1_11, ("w1", 1, 1))
+        first_layer(1, 0)
+        w1_20 = regroup("vector", rows[("w1", 2, 0)])
+        w1_21 = regroup("vector", rows[("w1", 2, 1)])
+        quantise(w1_20, ("w1", 2, 0))
+        quantise(w1_21, ("w1", 2, 1))
+        x_grouped = copy_x(transpose_x(1))
+        first_layer(2, 0)
+        h_00 = regroup("vector", h_rows[(0, 0)])
+        h_10 = regroup("vector", h_rows[(1, 0)])
+        quantise(x_grouped[0], ("x", 0, 1))
+        quantise(x_grouped[1], ("x", 1, 1))
+        first_layer(0, 1)
+        quantise(h_00, ("h", 0, 0))
+        quantise(h_10, ("h", 1, 0))
+        regroup_block(0, "vector", (0, 1))
+        first_layer(1, 1)
+        h_20 = regroup("vector", h_rows[(2, 0)])
+        regroup_block(0, "vector", (2,))
+        quantise(h_20, ("h", 2, 0))
+        regroup_block(0, "vector", (3, 4))
+        quantise_block(0)
+        first_layer(2, 1)
+        nc.scalar.activation(out=warm[:, 2:3], in_=h_rows[(2, 1)][:, 3, 0:1], func=ACT.Sigmoid)
 
-        g00 = regroup("v", raw[("w1", 0, 0)])
-        g01 = regroup("v", raw[("w1", 0, 1)])
-        quantise(g00, ("w1", 0, 0))
-        quantise(g01, ("w1", 0, 1))
-        gx = x_copies(x_transposes(0))
-        g10 = regroup("s", raw[("w1", 1, 0)])
-        quantise(gx[0], ("x", 0, 0))
-        quantise(gx[1], ("x", 1, 0))
-        layer1(0, 0)
-        g11 = regroup("v", raw[("w1", 1, 1)])
-        quantise(g10, ("w1", 1, 0))
-        quantise(g11, ("w1", 1, 1))
-        layer1(1, 0)
-        g20 = regroup("v", raw[("w1", 2, 0)])
-        g21 = regroup("v", raw[("w1", 2, 1)])
-        quantise(g20, ("w1", 2, 0))
-        quantise(g21, ("w1", 2, 1))
-        gx = x_copies(x_transposes(1))
-        layer1(2, 0)
-        h00 = regroup("v", hT[(0, 0)])
-        quantise(gx[0], ("x", 0, 1))
-        quantise(h00, ("h", 0, 0))
-        quantise(gx[1], ("x", 1, 1))
-        layer1(0, 1)
-        h10 = regroup("v", hT[(1, 0)])
-        block_part(0, "v", (0,))
-        quantise(h10, ("h", 1, 0))
-        block_part(0, "v", (1,))
-        layer1(1, 1)
-        h20 = regroup("v", hT[(2, 0)])
-        block_part(0, "v", (2,))
-        quantise(h20, ("h", 2, 0))
-        block_part(0, "v", (3, 4))
-        block_quantise(0)
-        layer1(2, 1)
-        nc.scalar.activation(out=warm[:, 2:3], in_=hT[(2, 1)][:, 3, 0:1], func=ACT.Sigmoid)
+        units = [(2 * b + t, c) for b in range(DIRECT) for c in range(2) for t in range(2)]
+        for unit in units[0:2]:
+            open_unit(*unit)
+            close_unit(*unit)
+        h_01 = regroup("vector", h_rows[(0, 1)])
+        h_11 = regroup("vector", h_rows[(1, 1)])
+        quantise(h_01, ("h", 0, 1))
+        quantise(h_11, ("h", 1, 1))
+        for unit in units[2:4]:
+            open_unit(*unit)
+        for unit in units[0:2]:
+            multiply_unit(*unit)
+        regroup_block(1, "scalar", (0, 1))
+        h_21 = regroup("vector", h_rows[(2, 1)])
+        regroup_block(1, "vector", (2,))
+        quantise(h_21, ("h", 2, 1))
+        store_pair(units[0:2])
+        regroup_block(1, "vector", (3, 4))
+        quantise_block(1)
 
-        units = [(2 * b + jj, c) for b in range(4) for c in range(2) for jj in range(2)]
-        for j, c in units[0:2]:
-            open_unit(j, c)
-            close_unit(j, c)
-        h01 = regroup("v", hT[(0, 1)])
-        h11 = regroup("v", hT[(1, 1)])
-        quantise(h01, ("h", 0, 1))
-        quantise(h11, ("h", 1, 1))
-        for j, c in units[2:4]:
-            open_unit(j, c)
-        for j, c in units[0:2]:
-            gate(j, c)
-        block_part(1, "s", (0, 1))
-        h21 = regroup("v", hT[(2, 1)])
-        block_part(1, "v", (2,))
-        quantise(h21, ("h", 2, 1))
-        finish(units[0:2])
-        block_part(1, "v", (3, 4))
-        block_quantise(1)
-
-        for n in range(2, 12):
-            j, c = units[n]
-            if n >= AHEAD:
-                open_unit(j, c)
-            close_unit(j, c)
-            gate(j, c)
+        for n in range(2, len(units)):
+            if n >= 4:
+                open_unit(*units[n])
+            close_unit(*units[n])
+            multiply_unit(*units[n])
             if n in (3, 7):
-                block_part(n // 4 + 2, "v", (0, 1, 2, 3, 4))
+                regroup_block((n + 5) // 4, "vector", range(SLICES))
             if n in (4, 8):
-                block_quantise(n // 4 + 1)
+                quantise_block((n + 4) // 4)
             if n % 2 == 1 and n >= 5:
-                finish(units[n - 3 : n - 1])
-        direct_group(3, 0)
-        finish(units[10:12])
-        direct_group(3, 1)
+                store_pair(units[n - 3 : n - 1])
+        direct_half(0)
+        store_pair(units[len(units) - 2 :])
+        direct_half(1)

@@ -17,6 +17,7 @@ P = 128
 PACK = 4
 CHUNK = 512
 BLOCK = 256
+SHARE = 192
 SLICES = 5
 DIRECT = 3
 B1_AT, B2G_AT, BV_AT, BIAS_TILES = 0, 12, 20, 28
@@ -35,6 +36,9 @@ def tile_selectivemixing_pa_kernel(tc, x, W1, b1, W2g, b2g, Wv, bv, out):
 
         def bank(shape, dtype, name):
             return psum.tile(shape, dtype, name=name, tag="bank")
+
+        def vbank(name):
+            return psum.tile([P, CHUNK], F32, name=name, tag="bank")
 
         bias_rows = const.tile([P, P], BF16, name="bias_rows")
         nc.vector.memset(bias_rows[:], 0.0)
@@ -77,11 +81,12 @@ def tile_selectivemixing_pa_kernel(tc, x, W1, b1, W2g, b2g, Wv, bv, out):
 
         for g in range(2):
             load_k_pairs(W1, "w1", 0, g)
-        for pair in (0, 1):
-            load_x(pair)
-        for chunk in (1, 2):
-            for g in range(2):
-                load_k_pairs(W1, "w1", chunk, g)
+        load_x(0)
+        load_k_pairs(W1, "w1", 1, 0)
+        load_x(1)
+        load_k_pairs(W1, "w1", 1, 1)
+        for g in range(2):
+            load_k_pairs(W1, "w1", 2, g)
         for pair in (2, 3):
             load_x(pair)
         for chunk in range(2):
@@ -114,6 +119,13 @@ def tile_selectivemixing_pa_kernel(tc, x, W1, b1, W2g, b2g, Wv, bv, out):
             side_by_side(engine, grouped[:], src[:])
             return grouped
 
+        def regroup_shared(src):
+            grouped = stage.tile([P, CHUNK, PACK], BF16, name="grouped", tag="grouped", align_bytes=64)
+            own = CHUNK - SHARE
+            side_by_side("scalar", grouped[:, own:, :], src[:, :, own:])
+            side_by_side("vector", grouped[:, :own, :], src[:, :, :own])
+            return grouped
+
         def quantise(grouped, key):
             name = "%s_%d_%d" % key
             words = keep.tile([P, CHUNK], U32, name="words_" + name, align_bytes=64)
@@ -124,6 +136,22 @@ def tile_selectivemixing_pa_kernel(tc, x, W1, b1, W2g, b2g, Wv, bv, out):
                 in_=grouped[:].rearrange("p w t -> p (w t)"),
             )
             mx[key] = (words[:], scales[:])
+
+        def x_words(c):
+            for g in range(2):
+                name = "x_%d_%d" % (g, c)
+                words = keep.tile([P, CHUNK], U32, name="words_" + name, align_bytes=64)
+                scales = keep.tile([P, CHUNK], U8, name="scales_" + name, align_bytes=64)
+                mx[("x", g, c)] = (words[:], scales[:])
+
+        def quantise_x_pair(grouped, g, c, pair):
+            cols = slice(pair * 256, (pair + 1) * 256)
+            words, scales = mx[("x", g, c)]
+            nc.vector.quantize_mx(
+                out=words[:, cols].bitcast(FP8X4),
+                scales=scales[:, cols],
+                in_=grouped[g][:, cols, :].rearrange("p w t -> p (w t)"),
+            )
 
         def mx_pass(acc, stationary, tile_index, moving, start, stop):
             cols = slice(tile_index * P, (tile_index + 1) * P)
@@ -137,9 +165,9 @@ def tile_selectivemixing_pa_kernel(tc, x, W1, b1, W2g, b2g, Wv, bv, out):
                 stop=stop,
             )
 
-        def transpose_x(c):
+        def transpose_x(c, pairs=(0, 1)):
             banks = []
-            for pair in range(2):
+            for pair in pairs:
                 x_words = x_tiles[2 * c + pair][:].bitcast(F32)
                 for g in range(2):
                     xt = bank([P, 2, 2 * P], F32, "xt")
@@ -154,12 +182,14 @@ def tile_selectivemixing_pa_kernel(tc, x, W1, b1, W2g, b2g, Wv, bv, out):
                     banks.append((pair, g, xt))
             return banks
 
-        def copy_x(banks):
-            grouped = {}
-            for g in range(2):
-                grouped[g] = stage.tile(
-                    [P, CHUNK, PACK], BF16, name="grouped_x", tag="grouped", align_bytes=64
-                )
+        def x_stage():
+            return [
+                stage.tile([P, CHUNK, PACK], BF16, name="grouped_x", tag="grouped", align_bytes=64)
+                for g in range(2)
+            ]
+
+        def copy_x(banks, grouped=None):
+            grouped = grouped or x_stage()
             for pair, g, xt in banks:
                 nc.scalar.copy(
                     out=grouped[g][:].bitcast(F32)[:, 2 * P * pair : 2 * P * (pair + 1), :],
@@ -183,6 +213,20 @@ def tile_selectivemixing_pa_kernel(tc, x, W1, b1, W2g, b2g, Wv, bv, out):
                     bias=bias_cols[:, at : at + 1], scale=1.0,
                 )
 
+        def first_layer_pair(pair, z):
+            cols = slice(pair * 256, (pair + 1) * 256)
+            for t in range(PACK):
+                for g in range(2):
+                    xw = mx[("x", g, 0)]
+                    mx_pass(z[t][:, cols], mx[("w1", 0, g)], t, (xw[0][:, cols], xw[1][:, cols]), g == 0, g == 1)
+
+        def silu_bank(g2, c, t, z):
+            at = B1_AT + PACK * g2 + t
+            nc.scalar.activation(
+                out=h_rows[(g2, c)][:, t, :], in_=z[:], func=ACT.Silu,
+                bias=bias_cols[:, at : at + 1], scale=1.0,
+            )
+
         block_grouped = {}
         block_mx = {}
 
@@ -201,16 +245,22 @@ def tile_selectivemixing_pa_kernel(tc, x, W1, b1, W2g, b2g, Wv, bv, out):
                 )
 
         def quantise_block(b):
+            quantise_slices(b, ((0, 4), (4, 5)))
+
+        def quantise_slices(b, parts):
             grouped = block_grouped[b]
-            words = keep.tile([P, SLICES, BLOCK], U32, name="words_block_%d" % b, align_bytes=64)
-            scales = keep.tile([P, SLICES, BLOCK], U8, name="scales_block_%d" % b, align_bytes=64)
-            for lo, hi in ((0, 4), (4, 5)):
+            if b in block_mx:
+                words, scales = block_mx[b]
+            else:
+                words = keep.tile([P, SLICES, BLOCK], U32, name="words_block_%d" % b, align_bytes=64)
+                scales = keep.tile([P, SLICES, BLOCK], U8, name="scales_block_%d" % b, align_bytes=64)
+                block_mx[b] = (words, scales)
+            for lo, hi in parts:
                 nc.vector.quantize_mx(
                     out=words[:, lo:hi, :].rearrange("p s w -> p (s w)").bitcast(FP8X4),
                     scales=scales[:, lo:hi, :].rearrange("p s w -> p (s w)"),
                     in_=grouped[:, lo:hi, :, :].rearrange("p s w t -> p (s w t)"),
                 )
-            block_mx[b] = (words, scales)
 
         def wv_slice(b, g):
             return (block_mx[b][0][:, g, :], block_mx[b][1][:, g, :])
@@ -218,26 +268,26 @@ def tile_selectivemixing_pa_kernel(tc, x, W1, b1, W2g, b2g, Wv, bv, out):
         def w2_slice(b, g):
             return (block_mx[b][0][:, 2 + g, :], block_mx[b][1][:, 2 + g, :])
 
-        sums = {}
-        gates = {}
-        products = {}
+        vsum, gsum, gates, products = {}, {}, {}, {}
 
-        def open_unit(j, c):
-            b, tile_index = j // 2, j % 2
-            v = bank([P, CHUNK], F32, "v")
+        def pass_v(j, c):
+            b, k = j // 2, j % 2
+            v = vbank("v")
             for g in range(2):
-                mx_pass(v[:], wv_slice(b, g), tile_index, mx[("x", g, c)], g == 0, g == 1)
-            gsum = bank([P, CHUNK], F32, "gsum")
-            for g in range(2):
-                mx_pass(gsum[:], w2_slice(b, g), tile_index, mx[("h", g, c)], g == 0, False)
-            sums[(j, c)] = (gsum, v)
+                mx_pass(v[:], wv_slice(b, g), k, mx[("x", g, c)], g == 0, g == 1)
+            vsum[(j, c)] = v
 
-        def close_unit(j, c):
-            gsum = sums[(j, c)][0]
-            mx_pass(gsum[:], w2_slice(j // 2, 2), j % 2, mx[("h", 2, c)], False, True)
+        def pass_g(j, c, gs=(0, 1, 2)):
+            b, k = j // 2, j % 2
+            if (j, c) not in gsum:
+                gsum[(j, c)] = bank([P, CHUNK], F32, "gsum")
+            for g in gs:
+                mx_pass(gsum[(j, c)][:], w2_slice(b, g), k, mx[("h", g, c)], g == 0, g == 2)
+
+        def gate(j, c):
             s = tail.tile([P, CHUNK], F32, name="gate", tag="gate")
             nc.scalar.activation(
-                out=s[:], in_=gsum[:], func=ACT.Sigmoid,
+                out=s[:], in_=gsum[(j, c)][:], func=ACT.Sigmoid,
                 bias=bias_cols[:, B2G_AT + j : B2G_AT + j + 1], scale=1.0,
             )
             gates[(j, c)] = s
@@ -245,32 +295,39 @@ def tile_selectivemixing_pa_kernel(tc, x, W1, b1, W2g, b2g, Wv, bv, out):
         def multiply_unit(j, c):
             prod = tail.tile([P, CHUNK], F32, name="product", tag="product", bufs=6)
             nc.vector.scalar_tensor_tensor(
-                out=prod[:], in0=sums[(j, c)][1][:], scalar=bias_cols[:, BV_AT + j : BV_AT + j + 1],
+                out=prod[:], in0=vsum[(j, c)][:], scalar=bias_cols[:, BV_AT + j : BV_AT + j + 1],
                 in1=gates[(j, c)][:], op0=ALU.add, op1=ALU.mult,
             )
             products[(j, c)] = prod
 
-        def store_pair(pair):
+        def back_pair(pair):
             banks = []
             for unit in pair:
                 back = bank([P, 4, P], F32, "back")
                 for r in range(4):
                     nc.tensor.transpose(back[:, r, :], products[unit][:, r * P : (r + 1) * P], ident_f32[:])
                 banks.append(back)
+            return banks
+
+        def out_pair(pair, banks):
             j, c = pair[0]
             result = tail.tile([P, 4, 2 * P], F32, name="result", tag="result")
             for k in range(2):
                 nc.scalar.copy(out=result[:, :, k * P : (k + 1) * P], in_=banks[k][:])
             nc.sync.dma_start(out=out_view[:, 4 * c : 4 * c + 4, j * P : (j + 2) * P], in_=result[:])
 
+        def store_pair(pair):
+            out_pair(pair, back_pair(pair))
+
         def direct_multiply(c, r, biased, s):
             result = tail.tile([P, BLOCK], F32, name="direct_result", tag="direct_result")
             nc.vector.tensor_tensor(out=result[:], in0=biased[:, 1, :], in1=s[:], op=ALU.mult)
             nc.sync.dma_start(out=out_view[:, 4 * c + r, direct_cols], in_=result[:])
 
-        def direct_half(c):
-            waiting = []
-            for r in range(4):
+        waiting = []
+
+        def direct_tiles(c, tiles):
+            for r in tiles:
                 gv = bank([P, 2, BLOCK], F32, "gv")
                 for g in range(3):
                     mx_pass(gv[:, 0, :], mx[("h", g, c)], r, w2_slice(DIRECT, g), g == 0, g == 2)
@@ -283,22 +340,35 @@ def tile_selectivemixing_pa_kernel(tc, x, W1, b1, W2g, b2g, Wv, bv, out):
                 waiting.append((r, biased, s))
                 if len(waiting) > 1:
                     direct_multiply(c, *waiting.pop(0))
-            direct_multiply(c, *waiting.pop(0))
+            if tiles[-1] == 3:
+                direct_multiply(c, *waiting.pop(0))
+
+        def direct_half(c):
+            direct_tiles(c, range(4))
 
         bias_t = bank([P, P], BF16, "bias_t")
         nc.tensor.transpose(bias_t[:], bias_rows[:], ident_bf16[:])
         bias_cols = const.tile([P, 32], F32, name="bias_cols")
-        nc.vector.tensor_copy(out=bias_cols[:, 0:BIAS_TILES], in_=bias_t[:, 0:BIAS_TILES])
 
-        w1_00 = regroup("vector", rows[("w1", 0, 0)])
-        w1_01 = regroup("vector", rows[("w1", 0, 1)])
+        w1_00 = regroup_shared(rows[("w1", 0, 0)])
+        w1_01 = regroup_shared(rows[("w1", 0, 1)])
         quantise(w1_00, ("w1", 0, 0))
+        nc.vector.tensor_copy(out=bias_cols[:, 0:BIAS_TILES], in_=bias_t[:, 0:BIAS_TILES])
         quantise(w1_01, ("w1", 0, 1))
-        x_grouped = copy_x(transpose_x(0))
-        w1_10 = regroup("scalar", rows[("w1", 1, 0)])
-        quantise(x_grouped[0], ("x", 0, 0))
-        quantise(x_grouped[1], ("x", 1, 0))
-        first_layer(0, 0)
+        x_words(0)
+        x_grouped = copy_x(transpose_x(0, (0,)))
+        h_rows[(0, 0)] = keep.tile([P, PACK, CHUNK], BF16, name="h_0_0", tag="rows_w1_0_0")
+        z0 = [bank([P, CHUNK], F32, "z") for t in range(PACK)]
+        w1_10 = regroup_shared(rows[("w1", 1, 0)])
+        quantise_x_pair(x_grouped, 0, 0, 0)
+        quantise_x_pair(x_grouped, 1, 0, 0)
+        copy_x(transpose_x(0, (1,)), x_grouped)
+        first_layer_pair(0, z0)
+        quantise_x_pair(x_grouped, 0, 0, 1)
+        quantise_x_pair(x_grouped, 1, 0, 1)
+        first_layer_pair(1, z0)
+        for t in range(PACK):
+            silu_bank(0, 0, t, z0[t])
         w1_11 = regroup("vector", rows[("w1", 1, 1)])
         quantise(w1_10, ("w1", 1, 0))
         quantise(w1_11, ("w1", 1, 1))
@@ -310,53 +380,81 @@ def tile_selectivemixing_pa_kernel(tc, x, W1, b1, W2g, b2g, Wv, bv, out):
         x_grouped = copy_x(transpose_x(1))
         first_layer(2, 0)
         h_00 = regroup("vector", h_rows[(0, 0)])
-        h_10 = regroup("vector", h_rows[(1, 0)])
         quantise(x_grouped[0], ("x", 0, 1))
         quantise(x_grouped[1], ("x", 1, 1))
         first_layer(0, 1)
+        h_10 = regroup("vector", h_rows[(1, 0)])
         quantise(h_00, ("h", 0, 0))
-        quantise(h_10, ("h", 1, 0))
         regroup_block(0, "vector", (0, 1))
         first_layer(1, 1)
+        quantise(h_10, ("h", 1, 0))
         h_20 = regroup("vector", h_rows[(2, 0)])
-        regroup_block(0, "vector", (2,))
+        regroup_block(0, "vector", (2, 3))
         quantise(h_20, ("h", 2, 0))
-        regroup_block(0, "vector", (3, 4))
+        regroup_block(0, "vector", (4,))
         quantise_block(0)
         first_layer(2, 1)
+        regroup_block(1, "scalar", (0, 1))
         nc.scalar.activation(out=warm[:, 2:3], in_=h_rows[(2, 1)][:, 3, 0:1], func=ACT.Sigmoid)
-
-        units = [(2 * b + t, c) for b in range(DIRECT) for c in range(2) for t in range(2)]
-        for unit in units[0:2]:
-            open_unit(*unit)
-            close_unit(*unit)
+        for j in range(2):
+            pass_v(j, 0)
+            pass_g(j, 0)
+            gate(j, 0)
         h_01 = regroup("vector", h_rows[(0, 1)])
+        regroup_block(1, "vector", (2, 3, 4))
+        for j in range(2):
+            pass_v(j, 1)
+        quantise_block(1)
         h_11 = regroup("vector", h_rows[(1, 1)])
         quantise(h_01, ("h", 0, 1))
+        multiply_unit(0, 0)
+        multiply_unit(1, 0)
+        for j in range(2, 4):
+            pass_v(j, 0)
+            pass_g(j, 0)
+            gate(j, 0)
         quantise(h_11, ("h", 1, 1))
-        for unit in units[2:4]:
-            open_unit(*unit)
-        for unit in units[0:2]:
-            multiply_unit(*unit)
-        regroup_block(1, "scalar", (0, 1))
         h_21 = regroup("vector", h_rows[(2, 1)])
-        regroup_block(1, "vector", (2,))
+        regroup_block(2, "scalar", (0,))
+        store_pair([(0, 0), (1, 0)])
+        regroup_block(2, "scalar", (1,))
+        for j in range(2):
+            pass_g(j, 1, (0, 1))
+        multiply_unit(2, 0)
         quantise(h_21, ("h", 2, 1))
-        store_pair(units[0:2])
-        regroup_block(1, "vector", (3, 4))
-        quantise_block(1)
-
-        for n in range(2, len(units)):
-            if n >= 4:
-                open_unit(*units[n])
-            close_unit(*units[n])
-            multiply_unit(*units[n])
-            if n in (3, 7):
-                regroup_block((n + 5) // 4, "vector", range(SLICES))
-            if n in (4, 8):
-                quantise_block((n + 4) // 4)
-            if n % 2 == 1 and n >= 5:
-                store_pair(units[n - 3 : n - 1])
-        direct_half(0)
-        store_pair(units[len(units) - 2 :])
-        direct_half(1)
+        multiply_unit(3, 0)
+        for j in range(2):
+            pass_g(j, 1, (2,))
+            gate(j, 1)
+        store_pair([(2, 0), (3, 0)])
+        regroup_block(2, "vector", (2, 3, 4))
+        for j in range(2):
+            multiply_unit(j, 1)
+        quantise_block(2)
+        for j in range(2, 4):
+            pass_v(j, 1)
+            pass_g(j, 1)
+            gate(j, 1)
+        store_pair([(0, 1), (1, 1)])
+        multiply_unit(2, 1)
+        multiply_unit(3, 1)
+        for j in range(4, 6):
+            pass_v(j, 0)
+            pass_g(j, 0)
+            gate(j, 0)
+        regroup_block(3, "scalar", (0,))
+        regroup_block(3, "vector", (1, 2, 3, 4))
+        store_pair([(2, 1), (3, 1)])
+        multiply_unit(4, 0)
+        multiply_unit(5, 0)
+        quantise_block(3)
+        for j in range(4, 6):
+            pass_v(j, 1)
+            pass_g(j, 1)
+            gate(j, 1)
+        store_pair([(4, 0), (5, 0)])
+        multiply_unit(4, 1)
+        multiply_unit(5, 1)
+        direct_tiles(0, range(4))
+        store_pair([(4, 1), (5, 1)])
+        direct_tiles(1, range(4))

@@ -110,8 +110,8 @@ def tile_selectivemixing_pa_kernel(tc, x, W1, b1, W2g, b2g, Wv, bv, out):
         def side_by_side(engine, dst, src):
             copy_on(
                 engine,
-                dst.rearrange("p (c i) t -> p c t i", i=4),
-                src.rearrange("p t (c i) -> p c t i", i=4),
+                dst.rearrange("p (c i) t -> p c t i", i=8),
+                src.rearrange("p t (c i) -> p c t i", i=8),
             )
 
         def regroup(engine, src):

@@ -79,11 +79,11 @@ def tile_selectivemixing_pa_kernel(tc, x, W1, b1, W2g, b2g, Wv, bv, out):
             nc.sync.dma_start(out=t[:], in_=view[g, :, :, chunk * CHUNK : (chunk + 1) * CHUNK])
             rows[(name, chunk, g)] = t
 
-        for g in range(2):
-            load_k_pairs(W1, "w1", 0, g)
+        load_k_pairs(W1, "w1", 0, 0)
         load_x(0)
-        load_k_pairs(W1, "w1", 1, 0)
+        load_k_pairs(W1, "w1", 0, 1)
         load_x(1)
+        load_k_pairs(W1, "w1", 1, 0)
         load_k_pairs(W1, "w1", 1, 1)
         for g in range(2):
             load_k_pairs(W1, "w1", 2, g)
@@ -321,7 +321,8 @@ def tile_selectivemixing_pa_kernel(tc, x, W1, b1, W2g, b2g, Wv, bv, out):
 
         def direct_multiply(c, r, biased, s):
             result = tail.tile([P, BLOCK], F32, name="direct_result", tag="direct_result")
-            nc.vector.tensor_tensor(out=result[:], in0=biased[:, 1, :], in1=s[:], op=ALU.mult)
+            engine = nc.vector if (c, r) == (1, 3) else nc.gpsimd
+            engine.tensor_tensor(out=result[:], in0=biased[:, 1, :], in1=s[:], op=ALU.mult)
             nc.sync.dma_start(out=out_view[:, 4 * c + r, direct_cols], in_=result[:])
 
         waiting = []
@@ -340,30 +341,44 @@ def tile_selectivemixing_pa_kernel(tc, x, W1, b1, W2g, b2g, Wv, bv, out):
                 waiting.append((r, biased, s))
                 if len(waiting) > 1:
                     direct_multiply(c, *waiting.pop(0))
-            if tiles[-1] == 3:
+            if tiles[-1] == 3 or (c, tiles[-1]) == (1, 2):
                 direct_multiply(c, *waiting.pop(0))
 
         def direct_half(c):
             direct_tiles(c, range(4))
 
+        def direct_last(c, r):
+            g_bank = bank([P, BLOCK], F32, "g_last")
+            for g in range(3):
+                mx_pass(g_bank[:], mx[("h", g, c)], r, w2_slice(DIRECT, g), g == 0, g == 2)
+            v_bank = bank([P, BLOCK], F32, "v_last")
+            for g in range(2):
+                mx_pass(v_bank[:], mx[("x", g, c)], r, wv_slice(DIRECT, g), g == 0, g == 1)
+            biased = tail.tile([P, 2, BLOCK], F32, name="biased", tag="product", bufs=6)
+            nc.vector.tensor_tensor(out=biased[:, 0, :], in0=g_bank[:], in1=bias_free[:, 0, :], op=ALU.add)
+            s = tail.tile([P, BLOCK], F32, name="direct_gate", tag="gate")
+            nc.scalar.activation(out=s[:], in_=biased[:, 0, :], func=ACT.Sigmoid)
+            nc.vector.tensor_tensor(out=biased[:, 1, :], in0=v_bank[:], in1=bias_free[:, 1, :], op=ALU.add)
+            direct_multiply(c, r, biased, s)
+
         bias_t = bank([P, P], BF16, "bias_t")
         nc.tensor.transpose(bias_t[:], bias_rows[:], ident_bf16[:])
         bias_cols = const.tile([P, 32], F32, name="bias_cols")
 
-        w1_00 = regroup_shared(rows[("w1", 0, 0)])
+        x_words(0)
+        w1_00 = regroup("vector", rows[("w1", 0, 0)])
+        nc.vector.tensor_copy(out=bias_cols[:, 0:BIAS_TILES], in_=bias_t[:, 0:BIAS_TILES])
+        x_grouped = copy_x(transpose_x(0, (0,)))
         w1_01 = regroup_shared(rows[("w1", 0, 1)])
         quantise(w1_00, ("w1", 0, 0))
-        nc.vector.tensor_copy(out=bias_cols[:, 0:BIAS_TILES], in_=bias_t[:, 0:BIAS_TILES])
+        quantise_x_pair(x_grouped, 0, 0, 0)
         quantise(w1_01, ("w1", 0, 1))
-        x_words(0)
-        x_grouped = copy_x(transpose_x(0, (0,)))
+        quantise_x_pair(x_grouped, 1, 0, 0)
         h_rows[(0, 0)] = keep.tile([P, PACK, CHUNK], BF16, name="h_0_0", tag="rows_w1_0_0")
         z0 = [bank([P, CHUNK], F32, "z") for t in range(PACK)]
-        w1_10 = regroup_shared(rows[("w1", 1, 0)])
-        quantise_x_pair(x_grouped, 0, 0, 0)
-        quantise_x_pair(x_grouped, 1, 0, 0)
         copy_x(transpose_x(0, (1,)), x_grouped)
         first_layer_pair(0, z0)
+        w1_10 = regroup_shared(rows[("w1", 1, 0)])
         quantise_x_pair(x_grouped, 0, 0, 1)
         quantise_x_pair(x_grouped, 1, 0, 1)
         first_layer_pair(1, z0)
@@ -457,4 +472,5 @@ def tile_selectivemixing_pa_kernel(tc, x, W1, b1, W2g, b2g, Wv, bv, out):
         multiply_unit(5, 1)
         direct_tiles(0, range(4))
         store_pair([(4, 1), (5, 1)])
-        direct_tiles(1, range(4))
+        direct_tiles(1, range(3))
+        direct_last(1, 3)

@@ -119,9 +119,9 @@ def tile_selectivemixing_pa_kernel(tc, x, W1, b1, W2g, b2g, Wv, bv, out):
             side_by_side(engine, grouped[:], src[:])
             return grouped
 
-        def regroup_shared(src):
+        def regroup_shared(src, share=SHARE):
             grouped = stage.tile([P, CHUNK, PACK], BF16, name="grouped", tag="grouped", align_bytes=64)
-            own = CHUNK - SHARE
+            own = CHUNK - share
             side_by_side("scalar", grouped[:, own:, :], src[:, :, own:])
             side_by_side("vector", grouped[:, :own, :], src[:, :, :own])
             return grouped
@@ -320,7 +320,7 @@ def tile_selectivemixing_pa_kernel(tc, x, W1, b1, W2g, b2g, Wv, bv, out):
             out_pair(pair, back_pair(pair))
 
         def direct_multiply(c, r, biased, s):
-            result = tail.tile([P, BLOCK], F32, name="direct_result", tag="direct_result")
+            result = tail.tile([P, BLOCK], F32, name="direct_result", tag="direct_result", bufs=8)
             engine = nc.vector if (c, r) == (1, 3) else nc.gpsimd
             engine.tensor_tensor(out=result[:], in0=biased[:, 1, :], in1=s[:], op=ALU.mult)
             nc.sync.dma_start(out=out_view[:, 4 * c + r, direct_cols], in_=result[:])
@@ -361,19 +361,19 @@ def tile_selectivemixing_pa_kernel(tc, x, W1, b1, W2g, b2g, Wv, bv, out):
             nc.vector.tensor_tensor(out=biased[:, 1, :], in0=v_bank[:], in1=bias_free[:, 1, :], op=ALU.add)
             direct_multiply(c, r, biased, s)
 
+        x_words(0)
+        w1_00 = regroup("vector", rows[("w1", 0, 0)])
+        xt_banks = transpose_x(0, (0,))
         bias_t = bank([P, P], BF16, "bias_t")
         nc.tensor.transpose(bias_t[:], bias_rows[:], ident_bf16[:])
         bias_cols = const.tile([P, 32], F32, name="bias_cols")
-
-        x_words(0)
-        w1_00 = regroup("vector", rows[("w1", 0, 0)])
-        nc.vector.tensor_copy(out=bias_cols[:, 0:BIAS_TILES], in_=bias_t[:, 0:BIAS_TILES])
-        x_grouped = copy_x(transpose_x(0, (0,)))
+        x_grouped = copy_x(xt_banks)
         w1_01 = regroup_shared(rows[("w1", 0, 1)])
         quantise(w1_00, ("w1", 0, 0))
         quantise_x_pair(x_grouped, 0, 0, 0)
         quantise(w1_01, ("w1", 0, 1))
         quantise_x_pair(x_grouped, 1, 0, 0)
+        nc.vector.tensor_copy(out=bias_cols[:, 0:BIAS_TILES], in_=bias_t[:, 0:BIAS_TILES])
         h_rows[(0, 0)] = keep.tile([P, PACK, CHUNK], BF16, name="h_0_0", tag="rows_w1_0_0")
         z0 = [bank([P, CHUNK], F32, "z") for t in range(PACK)]
         copy_x(transpose_x(0, (1,)), x_grouped)
@@ -420,19 +420,18 @@ def tile_selectivemixing_pa_kernel(tc, x, W1, b1, W2g, b2g, Wv, bv, out):
         for j in range(2):
             pass_v(j, 1)
         quantise_block(1)
-        h_11 = regroup("vector", h_rows[(1, 1)])
+        h_11 = regroup_shared(h_rows[(1, 1)])
         quantise(h_01, ("h", 0, 1))
         multiply_unit(0, 0)
         multiply_unit(1, 0)
+        h_21 = regroup_shared(h_rows[(2, 1)])
         for j in range(2, 4):
             pass_v(j, 0)
             pass_g(j, 0)
             gate(j, 0)
         quantise(h_11, ("h", 1, 1))
-        h_21 = regroup("vector", h_rows[(2, 1)])
         regroup_block(2, "scalar", (0,))
         store_pair([(0, 0), (1, 0)])
-        regroup_block(2, "scalar", (1,))
         for j in range(2):
             pass_g(j, 1, (0, 1))
         multiply_unit(2, 0)
@@ -442,7 +441,7 @@ def tile_selectivemixing_pa_kernel(tc, x, W1, b1, W2g, b2g, Wv, bv, out):
             pass_g(j, 1, (2,))
             gate(j, 1)
         store_pair([(2, 0), (3, 0)])
-        regroup_block(2, "vector", (2, 3, 4))
+        regroup_block(2, "vector", (1, 2, 3, 4))
         for j in range(2):
             multiply_unit(j, 1)
         quantise_block(2)
@@ -459,7 +458,6 @@ def tile_selectivemixing_pa_kernel(tc, x, W1, b1, W2g, b2g, Wv, bv, out):
             gate(j, 0)
         regroup_block(3, "scalar", (0,))
         regroup_block(3, "vector", (1, 2, 3, 4))
-        store_pair([(2, 1), (3, 1)])
         multiply_unit(4, 0)
         multiply_unit(5, 0)
         quantise_block(3)
@@ -467,7 +465,9 @@ def tile_selectivemixing_pa_kernel(tc, x, W1, b1, W2g, b2g, Wv, bv, out):
             pass_v(j, 1)
             pass_g(j, 1)
             gate(j, 1)
-        store_pair([(4, 0), (5, 0)])
+        stores = [back_pair([(2, 1), (3, 1)]), back_pair([(4, 0), (5, 0)])]
+        out_pair([(2, 1), (3, 1)], stores[0])
+        out_pair([(4, 0), (5, 0)], stores[1])
         multiply_unit(4, 1)
         multiply_unit(5, 1)
         direct_tiles(0, range(4))

@@ -368,8 +368,8 @@ def tile_selectivemixing_pa_kernel(tc, x, W1, b1, W2g, b2g, Wv, bv, out):
         nc.tensor.transpose(bias_t[:], bias_rows[:], ident_bf16[:])
         bias_cols = const.tile([P, 32], F32, name="bias_cols")
         x_grouped = copy_x(xt_banks)
-        w1_01 = regroup_shared(rows[("w1", 0, 1)])
         quantise(w1_00, ("w1", 0, 0))
+        w1_01 = regroup_shared(rows[("w1", 0, 1)], 128)
         quantise_x_pair(x_grouped, 0, 0, 0)
         quantise(w1_01, ("w1", 0, 1))
         quantise_x_pair(x_grouped, 1, 0, 0)
@@ -378,7 +378,7 @@ def tile_selectivemixing_pa_kernel(tc, x, W1, b1, W2g, b2g, Wv, bv, out):
         z0 = [bank([P, CHUNK], F32, "z") for t in range(PACK)]
         copy_x(transpose_x(0, (1,)), x_grouped)
         first_layer_pair(0, z0)
-        w1_10 = regroup_shared(rows[("w1", 1, 0)])
+        w1_10 = regroup_shared(rows[("w1", 1, 0)], 256)
         quantise_x_pair(x_grouped, 0, 0, 1)
         quantise_x_pair(x_grouped, 1, 0, 1)
         first_layer_pair(1, z0)
@@ -420,9 +420,9 @@ def tile_selectivemixing_pa_kernel(tc, x, W1, b1, W2g, b2g, Wv, bv, out):
         for j in range(2):
             pass_v(j, 1)
         quantise_block(1)
-        h_11 = regroup_shared(h_rows[(1, 1)])
         quantise(h_01, ("h", 0, 1))
         multiply_unit(0, 0)
+        h_11 = regroup_shared(h_rows[(1, 1)])
         multiply_unit(1, 0)
         h_21 = regroup_shared(h_rows[(2, 1)])
         for j in range(2, 4):

@@ -44,13 +44,11 @@ def tile_selectivemixing_pa_kernel(tc, x, W1, b1, W2g, b2g, Wv, bv, out):
         nc.vector.memset(bias_rows[:], 0.0)
         warm = const.tile([P, 4], F32, name="warm")
         nc.vector.memset(warm[:], 0.0)
-        for vec, at, end in ((b1, B1_AT, B2G_AT), (b2g, B2G_AT, BV_AT), (bv, BV_AT, BIAS_TILES)):
-            nc.scalar.dma_start(out=bias_rows[at:end, :], in_=vec.rearrange("(j p) -> j p", p=P))
         nc.scalar.activation(out=warm[:, 1:2], in_=warm[:, 0:1], func=ACT.Silu)
-        ident_bf16 = const.tile([P, P], BF16, name="ident_bf16")
-        masks.make_identity(nc, ident_bf16[:])
         ident_f32 = const.tile([P, P], F32, name="ident_f32")
         masks.make_identity(nc, ident_f32[:])
+        ident_bf16 = const.tile([P, P], BF16, name="ident_bf16")
+        masks.make_identity(nc, ident_bf16[:])
 
         x_view = x.flatten_outer_dims().rearrange("(p i) k -> p i k", i=8)
         out_view = out.flatten_outer_dims().rearrange("(p i) d -> p i d", i=8)
@@ -83,6 +81,11 @@ def tile_selectivemixing_pa_kernel(tc, x, W1, b1, W2g, b2g, Wv, bv, out):
         load_x(0)
         load_k_pairs(W1, "w1", 0, 1)
         load_x(1)
+        for vec, first, last, at in ((b1, 0, 8, B1_AT), (b1, 8, 12, B1_AT), (b2g, 0, 8, B2G_AT), (bv, 0, 8, BV_AT)):
+            nc.sync.dma_start(
+                out=bias_rows[at + first : at + last, :],
+                in_=vec.rearrange("(j p) -> j p", p=P)[first:last, :],
+            )
         load_k_pairs(W1, "w1", 1, 0)
         load_k_pairs(W1, "w1", 1, 1)
         for g in range(2):
@@ -364,23 +367,24 @@ def tile_selectivemixing_pa_kernel(tc, x, W1, b1, W2g, b2g, Wv, bv, out):
         x_words(0)
         w1_00 = regroup("vector", rows[("w1", 0, 0)])
         xt_banks = transpose_x(0, (0,))
-        bias_t = bank([P, P], BF16, "bias_t")
-        nc.tensor.transpose(bias_t[:], bias_rows[:], ident_bf16[:])
-        bias_cols = const.tile([P, 32], F32, name="bias_cols")
         x_grouped = copy_x(xt_banks)
         quantise(w1_00, ("w1", 0, 0))
         w1_01 = regroup_shared(rows[("w1", 0, 1)], 128)
         quantise_x_pair(x_grouped, 0, 0, 0)
         quantise(w1_01, ("w1", 0, 1))
         quantise_x_pair(x_grouped, 1, 0, 0)
-        nc.vector.tensor_copy(out=bias_cols[:, 0:BIAS_TILES], in_=bias_t[:, 0:BIAS_TILES])
         h_rows[(0, 0)] = keep.tile([P, PACK, CHUNK], BF16, name="h_0_0", tag="rows_w1_0_0")
         z0 = [bank([P, CHUNK], F32, "z") for t in range(PACK)]
-        copy_x(transpose_x(0, (1,)), x_grouped)
+        xt_banks = transpose_x(0, (1,))
+        bias_t = bank([P, P], BF16, "bias_t")
+        nc.tensor.transpose(bias_t[:], bias_rows[:], ident_bf16[:])
+        bias_cols = const.tile([P, 32], F32, name="bias_cols")
+        copy_x(xt_banks, x_grouped)
         first_layer_pair(0, z0)
         w1_10 = regroup_shared(rows[("w1", 1, 0)], 256)
         quantise_x_pair(x_grouped, 0, 0, 1)
         quantise_x_pair(x_grouped, 1, 0, 1)
+        nc.vector.tensor_copy(out=bias_cols[:, 0:BIAS_TILES], in_=bias_t[:, 0:BIAS_TILES])
         first_layer_pair(1, z0)
         for t in range(PACK):
             silu_bank(0, 0, t, z0[t])

@@ -322,35 +322,19 @@ def tile_selectivemixing_pa_kernel(tc, x, W1, b1, W2g, b2g, Wv, bv, out):
         def store_pair(pair):
             out_pair(pair, back_pair(pair))
 
-        def direct_multiply(c, r, biased, s):
-            result = tail.tile([P, BLOCK], F32, name="direct_result", tag="direct_result", bufs=8)
-            engine = nc.vector if (c, r) == (1, 3) else nc.gpsimd
-            engine.tensor_tensor(out=result[:], in0=biased[:, 1, :], in1=s[:], op=ALU.mult)
-            nc.sync.dma_start(out=out_view[:, 4 * c + r, direct_cols], in_=result[:])
+        def direct_tile(c, r):
+            gv = bank([P, 2, BLOCK], F32, "gv")
+            for g in range(3):
+                mx_pass(gv[:, 0, :], mx[("h", g, c)], r, w2_slice(DIRECT, g), g == 0, g == 2)
+            for g in range(2):
+                mx_pass(gv[:, 1, :], mx[("x", g, c)], r, wv_slice(DIRECT, g), g == 0, g == 1)
+            biased = tail.tile([P, 2, BLOCK], F32, name="biased", tag="product", bufs=6)
+            nc.vector.tensor_tensor(out=biased[:], in0=gv[:], in1=bias_free[:], op=ALU.add)
+            s = tail.tile([P, BLOCK], F32, name="direct_gate", tag="gate")
+            nc.scalar.activation(out=s[:], in_=biased[:, 0, :], func=ACT.Sigmoid)
+            return biased, s
 
-        waiting = []
-
-        def direct_tiles(c, tiles):
-            for r in tiles:
-                gv = bank([P, 2, BLOCK], F32, "gv")
-                for g in range(3):
-                    mx_pass(gv[:, 0, :], mx[("h", g, c)], r, w2_slice(DIRECT, g), g == 0, g == 2)
-                for g in range(2):
-                    mx_pass(gv[:, 1, :], mx[("x", g, c)], r, wv_slice(DIRECT, g), g == 0, g == 1)
-                biased = tail.tile([P, 2, BLOCK], F32, name="biased", tag="product", bufs=6)
-                nc.vector.tensor_tensor(out=biased[:], in0=gv[:], in1=bias_free[:], op=ALU.add)
-                s = tail.tile([P, BLOCK], F32, name="direct_gate", tag="gate")
-                nc.scalar.activation(out=s[:], in_=biased[:, 0, :], func=ACT.Sigmoid)
-                waiting.append((r, biased, s))
-                if len(waiting) > 1:
-                    direct_multiply(c, *waiting.pop(0))
-            if tiles[-1] == 3 or (c, tiles[-1]) == (1, 2):
-                direct_multiply(c, *waiting.pop(0))
-
-        def direct_half(c):
-            direct_tiles(c, range(4))
-
-        def direct_last(c, r):
+        def direct_last_tile(c, r):
             g_bank = bank([P, BLOCK], F32, "g_last")
             for g in range(3):
                 mx_pass(g_bank[:], mx[("h", g, c)], r, w2_slice(DIRECT, g), g == 0, g == 2)
@@ -362,7 +346,13 @@ def tile_selectivemixing_pa_kernel(tc, x, W1, b1, W2g, b2g, Wv, bv, out):
             s = tail.tile([P, BLOCK], F32, name="direct_gate", tag="gate")
             nc.scalar.activation(out=s[:], in_=biased[:, 0, :], func=ACT.Sigmoid)
             nc.vector.tensor_tensor(out=biased[:, 1, :], in0=v_bank[:], in1=bias_free[:, 1, :], op=ALU.add)
-            direct_multiply(c, r, biased, s)
+            return biased, s
+
+        def direct_multiply(engine, queue, c, r, tile):
+            biased, s = tile
+            result = tail.tile([P, BLOCK], F32, name="direct_result", tag="direct_result", bufs=8)
+            engine.tensor_tensor(out=result[:], in0=biased[:, 1, :], in1=s[:], op=ALU.mult)
+            queue.dma_start(out=out_view[:, 4 * c + r, direct_cols], in_=result[:])
 
         x_words(0)
         w1_00 = regroup("vector", rows[("w1", 0, 0)])
@@ -474,7 +464,13 @@ def tile_selectivemixing_pa_kernel(tc, x, W1, b1, W2g, b2g, Wv, bv, out):
         out_pair([(4, 0), (5, 0)], stores[1])
         multiply_unit(4, 1)
         multiply_unit(5, 1)
-        direct_tiles(0, range(4))
+        tiles = [direct_tile(0, r) for r in range(4)]
+        for r in range(4):
+            direct_multiply(nc.gpsimd if r < 3 else nc.vector, nc.sync, 0, r, tiles[r])
         store_pair([(4, 1), (5, 1)])
-        direct_tiles(1, range(3))
-        direct_last(1, 3)
+        tiles = [direct_tile(1, r) for r in range(3)]
+        direct_multiply(nc.gpsimd, nc.sync, 1, 0, tiles[0])
+        last = direct_last_tile(1, 3)
+        direct_multiply(nc.vector, nc.sync, 1, 1, tiles[1])
+        direct_multiply(nc.gpsimd, nc.sync, 1, 2, tiles[2])
+        direct_multiply(nc.vector, nc.scalar, 1, 3, last)

@@ -122,6 +122,18 @@ def tile_selectivemixing_pa_kernel(tc, x, W1, b1, W2g, b2g, Wv, bv, out):
             side_by_side(engine, grouped[:], src[:])
             return grouped
 
+        def regroup_by_tensor(dst, src):
+            for first in range(0, dst.shape[1], BLOCK):
+                woven = bank([P, BLOCK, PACK], BF16, "woven")
+                for half in range(2):
+                    cols = slice(half * P, (half + 1) * P)
+                    nc.tensor.matmul(
+                        woven[:, cols, :].rearrange("p c t -> p (c t)"), lhsT=ident_bf16[:],
+                        rhs=src[:, :, first + half * P : first + (half + 1) * P].rearrange("p t c -> p c t"),
+                        start=True, stop=True,
+                    )
+                nc.scalar.copy(out=dst[:, first : first + BLOCK, :], in_=woven[:])
+
         def regroup_shared(src, share=SHARE):
             grouped = stage.tile([P, CHUNK, PACK], BF16, name="grouped", tag="grouped", align_bytes=64)
             own = CHUNK - share
@@ -241,6 +253,11 @@ def tile_selectivemixing_pa_kernel(tc, x, W1, b1, W2g, b2g, Wv, bv, out):
                 )
             sources = [rows[("wv", chunk, g)] for g in range(2)] + [rows[("w2", chunk, g)] for g in range(3)]
             for s in slices:
+                if engine == "tensor":
+                    regroup_by_tensor(
+                        block_grouped[b][:, s, :, :], sources[s][:, :, part * BLOCK : (part + 1) * BLOCK]
+                    )
+                    continue
                 side_by_side(
                     engine,
                     block_grouped[b][:, s, :, :],
@@ -403,7 +420,7 @@ def tile_selectivemixing_pa_kernel(tc, x, W1, b1, W2g, b2g, Wv, bv, out):
         regroup_block(0, "vector", (4,))
         quantise_block(0)
         first_layer(2, 1)
-        regroup_block(1, "scalar", (0, 1))
+        regroup_block(1, "tensor", (0, 1))
         nc.scalar.activation(out=warm[:, 2:3], in_=h_rows[(2, 1)][:, 3, 0:1], func=ACT.Sigmoid)
         for j in range(2):
             pass_v(j, 0)
@@ -416,9 +433,9 @@ def tile_selectivemixing_pa_kernel(tc, x, W1, b1, W2g, b2g, Wv, bv, out):
         quantise_block(1)
         quantise(h_01, ("h", 0, 1))
         multiply_unit(0, 0)
-        h_11 = regroup_shared(h_rows[(1, 1)])
+        h_11 = regroup_shared(h_rows[(1, 1)], 256)
         multiply_unit(1, 0)
-        h_21 = regroup_shared(h_rows[(2, 1)])
+        h_21 = regroup_shared(h_rows[(2, 1)], 256)
         for j in range(2, 4):
             pass_v(j, 0)
             pass_g(j, 0)
@@ -466,11 +483,11 @@ def tile_selectivemixing_pa_kernel(tc, x, W1, b1, W2g, b2g, Wv, bv, out):
         multiply_unit(5, 1)
         tiles = [direct_tile(0, r) for r in range(4)]
         for r in range(4):
-            direct_multiply(nc.gpsimd if r < 3 else nc.vector, nc.sync, 0, r, tiles[r])
+            direct_multiply(nc.gpsimd, nc.sync, 0, r, tiles[r])
         store_pair([(4, 1), (5, 1)])
         tiles = [direct_tile(1, r) for r in range(3)]
-        direct_multiply(nc.gpsimd, nc.sync, 1, 0, tiles[0])
+        for r in range(2):
+            direct_multiply(nc.gpsimd, nc.sync, 1, r, tiles[r])
         last = direct_last_tile(1, 3)
-        direct_multiply(nc.vector, nc.sync, 1, 1, tiles[1])
-        direct_multiply(nc.gpsimd, nc.sync, 1, 2, tiles[2])
-        direct_multiply(nc.vector, nc.scalar, 1, 3, last)
+        direct_multiply(nc.vector, nc.sync, 1, 2, tiles[2])
+        direct_multiply(nc.vector, nc.sync, 1, 3, last)

@@ -143,8 +143,8 @@ def tile_selectivemixing_pa_kernel(tc, x, W1, b1, W2g, b2g, Wv, bv, out):
 
         def quantise(grouped, key):
             name = "%s_%d_%d" % key
-            words = keep.tile([P, CHUNK], U32, name="words_" + name, align_bytes=64)
-            scales = keep.tile([P, CHUNK], U8, name="scales_" + name, align_bytes=64)
+            words = keep.tile([P, CHUNK], U32, name="words_" + name, align_bytes=256)
+            scales = keep.tile([P, CHUNK], U8, name="scales_" + name, align_bytes=256)
             nc.vector.quantize_mx(
                 out=words[:].bitcast(FP8X4),
                 scales=scales[:],
@@ -155,8 +155,8 @@ def tile_selectivemixing_pa_kernel(tc, x, W1, b1, W2g, b2g, Wv, bv, out):
         def x_words(c):
             for g in range(2):
                 name = "x_%d_%d" % (g, c)
-                words = keep.tile([P, CHUNK], U32, name="words_" + name, align_bytes=64)
-                scales = keep.tile([P, CHUNK], U8, name="scales_" + name, align_bytes=64)
+                words = keep.tile([P, CHUNK], U32, name="words_" + name, align_bytes=256)
+                scales = keep.tile([P, CHUNK], U8, name="scales_" + name, align_bytes=256)
                 mx[("x", g, c)] = (words[:], scales[:])
 
         def quantise_x_pair(grouped, g, c, pair):
@@ -272,8 +272,8 @@ def tile_selectivemixing_pa_kernel(tc, x, W1, b1, W2g, b2g, Wv, bv, out):
             if b in block_mx:
                 words, scales = block_mx[b]
             else:
-                words = keep.tile([P, SLICES, BLOCK], U32, name="words_block_%d" % b, align_bytes=64)
-                scales = keep.tile([P, SLICES, BLOCK], U8, name="scales_block_%d" % b, align_bytes=64)
+                words = keep.tile([P, SLICES, BLOCK], U32, name="words_block_%d" % b, align_bytes=256)
+                scales = keep.tile([P, SLICES, BLOCK], U8, name="scales_block_%d" % b, align_bytes=256)
                 block_mx[b] = (words, scales)
             for lo, hi in parts:
                 nc.vector.quantize_mx(

from contextlib import ExitStack

import concourse.masks as masks
import concourse.mybir as mybir

FLOPS = 2 * 1024 * (1024 * 1536 + 1536 * 1024 + 1024 * 1024)

F32 = mybir.dt.float32
BF16 = mybir.dt.bfloat16
U32 = mybir.dt.uint32
U8 = mybir.dt.uint8
FP8X4 = mybir.dt.float8_e4m3fn_x4
ACT = mybir.ActivationFunctionType
ALU = mybir.AluOpType

P = 128
PACK = 4
CHUNK = 512
BLOCK = 256
SHARE = 192
SLICES = 5
DIRECT = 3
B1_AT, B2G_AT, BV_AT, BIAS_TILES = 0, 12, 20, 28


def tile_selectivemixing_pa_kernel(tc, x, W1, b1, W2g, b2g, Wv, bv, out):
    nc = tc.nc
    with ExitStack() as ctx:
        ctx.enter_context(tc.manual_schedule())
        const = ctx.enter_context(tc.tile_pool(name="const", bufs=1))
        keep = ctx.enter_context(tc.tile_pool(name="keep", bufs=1))
        stage = ctx.enter_context(tc.tile_pool(name="stage", bufs=4))
        wide = ctx.enter_context(tc.tile_pool(name="wide", bufs=2))
        tail = ctx.enter_context(tc.tile_pool(name="tail", bufs=4))
        psum = ctx.enter_context(tc.psum_pool(name="psum", bufs=8))

        def bank(shape, dtype, name):
            return psum.tile(shape, dtype, name=name, tag="bank")

        def vbank(name):
            return psum.tile([P, CHUNK], F32, name=name, tag="bank")

        bias_rows = const.tile([P, P], BF16, name="bias_rows")
        nc.vector.memset(bias_rows[:], 0.0)
        warm = const.tile([P, 4], F32, name="warm")
        nc.vector.memset(warm[:], 0.0)
        nc.scalar.activation(out=warm[:, 1:2], in_=warm[:, 0:1], func=ACT.Silu)
        ident_f32 = const.tile([P, P], F32, name="ident_f32")
        masks.make_identity(nc, ident_f32[:])
        ident_bf16 = const.tile([P, P], BF16, name="ident_bf16")
        masks.make_identity(nc, ident_bf16[:])

        x_view = x.flatten_outer_dims().rearrange("(p i) k -> p i k", i=8)
        out_view = out.flatten_outer_dims().rearrange("(p i) d -> p i d", i=8)
        x_tiles = {}
        rows = {}

        def load_x(pair):
            t = keep.tile([P, 2, 1024], BF16, name="x_%d" % pair)
            nc.sync.dma_start(out=t[:], in_=x_view[:, 2 * pair : 2 * pair + 2, :])
            x_tiles[pair] = t

        def load_k_pairs(W, name, chunk, g):
            view = W.rearrange("(a p e) f -> e p a f", a=4, p=P, e=2)
            t = keep.tile([P, PACK, CHUNK], BF16, name="rows_%s_%d_%d" % (name, chunk, g))
            by_e = t[:].rearrange("p (u e) f -> p u e f", e=2)
            for e in range(2):
                nc.sync.dma_start(
                    out=by_e[:, :, e, :],
                    in_=view[e, :, 2 * g : 2 * g + 2, chunk * CHUNK : (chunk + 1) * CHUNK],
                )
            rows[(name, chunk, g)] = t

        def load_k_rows(W, name, chunk, g):
            view = W.rearrange("(g t p) n -> g p t n", g=3, t=PACK, p=P)
            t = keep.tile([P, PACK, CHUNK], BF16, name="rows_%s_%d_%d" % (name, chunk, g))
            nc.sync.dma_start(out=t[:], in_=view[g, :, :, chunk * CHUNK : (chunk + 1) * CHUNK])
            rows[(name, chunk, g)] = t

        load_k_pairs(W1, "w1", 0, 0)
        load_x(0)
        load_k_pairs(W1, "w1", 0, 1)
        load_x(1)
        for vec, first, last, at in ((b1, 0, 8, B1_AT), (b1, 8, 12, B1_AT), (b2g, 0, 8, B2G_AT), (bv, 0, 8, BV_AT)):
            nc.sync.dma_start(
                out=bias_rows[at + first : at + last, :],
                in_=vec.rearrange("(j p) -> j p", p=P)[first:last, :],
            )
        load_k_pairs(W1, "w1", 1, 0)
        load_k_pairs(W1, "w1", 1, 1)
        for g in range(2):
            load_k_pairs(W1, "w1", 2, g)
        for pair in (2, 3):
            load_x(pair)
        for chunk in range(2):
            for g in range(2):
                load_k_pairs(Wv, "wv", chunk, g)
            for g in range(3):
                load_k_rows(W2g, "w2", chunk, g)
        bias_free = const.tile([P, 2, BLOCK], BF16, name="bias_free")
        direct_cols = slice(DIRECT * BLOCK, (DIRECT + 1) * BLOCK)
        nc.sync.dma_start(out=bias_free[:, 0, :], in_=b2g[direct_cols].partition_broadcast(P))
        nc.sync.dma_start(out=bias_free[:, 1, :], in_=bv[direct_cols].partition_broadcast(P))

        mx = {}

        def copy_on(engine, dst, src):
            if engine == "vector":
                nc.vector.tensor_copy(out=dst, in_=src)
            else:
                nc.scalar.copy(out=dst, in_=src)

        def side_by_side(engine, dst, src):
            copy_on(
                engine,
                dst.rearrange("p (c i) t -> p c t i", i=8),
                src.rearrange("p t (c i) -> p c t i", i=8),
            )

        def regroup(engine, src):
            grouped = stage.tile([P, CHUNK, PACK], BF16, name="grouped", tag="grouped", align_bytes=64)
            side_by_side(engine, grouped[:], src[:])
            return grouped

        def regroup_by_tensor(dst, src):
            for first in range(0, dst.shape[1], BLOCK):
                woven = bank([P, BLOCK, PACK], BF16, "woven")
                for half in range(2):
                    cols = slice(half * P, (half + 1) * P)
                    nc.tensor.matmul(
                        woven[:, cols, :].rearrange("p c t -> p (c t)"), lhsT=ident_bf16[:],
                        rhs=src[:, :, first + half * P : first + (half + 1) * P].rearrange("p t c -> p c t"),
                        start=True, stop=True,
                    )
                nc.scalar.copy(out=dst[:, first : first + BLOCK, :], in_=woven[:])

        def regroup_shared(src, share=SHARE):
            grouped = stage.tile([P, CHUNK, PACK], BF16, name="grouped", tag="grouped", align_bytes=64)
            own = CHUNK - share
            side_by_side("scalar", grouped[:, own:, :], src[:, :, own:])
            side_by_side("vector", grouped[:, :own, :], src[:, :, :own])
            return grouped

        def quantise(grouped, key):
            name = "%s_%d_%d" % key
            words = keep.tile([P, CHUNK], U32, name="words_" + name, align_bytes=256)
            scales = keep.tile([P, CHUNK], U8, name="scales_" + name, align_bytes=256)
            nc.vector.quantize_mx(
                out=words[:].bitcast(FP8X4),
                scales=scales[:],
                in_=grouped[:].rearrange("p w t -> p (w t)"),
            )
            mx[key] = (words[:], scales[:])

        def x_words(c):
            for g in range(2):
                name = "x_%d_%d" % (g, c)
                words = keep.tile([P, CHUNK], U32, name="words_" + name, align_bytes=256)
                scales = keep.tile([P, CHUNK], U8, name="scales_" + name, align_bytes=256)
                mx[("x", g, c)] = (words[:], scales[:])

        def quantise_x_pair(grouped, g, c, pair):
            cols = slice(pair * 256, (pair + 1) * 256)
            words, scales = mx[("x", g, c)]
            nc.vector.quantize_mx(
                out=words[:, cols].bitcast(FP8X4),
                scales=scales[:, cols],
                in_=grouped[g][:, cols, :].rearrange("p w t -> p (w t)"),
            )

        def mx_pass(acc, stationary, tile_index, moving, start, stop):
            cols = slice(tile_index * P, (tile_index + 1) * P)
            nc.tensor.matmul_mx(
                out=acc,
                lhsT=stationary[0][:, cols].bitcast(FP8X4),
                lhsT_scale=stationary[1][:, cols],
                rhs=moving[0].bitcast(FP8X4),
                rhs_scale=moving[1],
                start=start,
                stop=stop,
            )

        def transpose_x(c, pairs=(0, 1)):
            banks = []
            for pair in pairs:
                x_words = x_tiles[2 * c + pair][:].bitcast(F32)
                for g in range(2):
                    xt = bank([P, 2, 2 * P], F32, "xt")
                    for u in range(2):
                        for i in range(2):
                            first = 256 * g + 128 * u
                            nc.tensor.transpose(
                                xt[:, u, i * P : (i + 1) * P],
                                x_words[:, i, first : first + P],
                                ident_f32[:],
                            )
                    banks.append((pair, g, xt))
            return banks

        def x_stage():
            return [
                stage.tile([P, CHUNK, PACK], BF16, name="grouped_x", tag="grouped", align_bytes=64)
                for g in range(2)
            ]

        def copy_x(banks, grouped=None):
            grouped = grouped or x_stage()
            for pair, g, xt in banks:
                nc.scalar.copy(
                    out=grouped[g][:].bitcast(F32)[:, 2 * P * pair : 2 * P * (pair + 1), :],
                    in_=xt[:].rearrange("p u r -> p r u"),
                )
            return grouped

        h_rows = {}

        def first_layer(g2, c):
            h_rows[(g2, c)] = keep.tile(
                [P, PACK, CHUNK], BF16, name="h_%d_%d" % (g2, c), tag="rows_w1_%d_%d" % (g2, c)
            )
            for t in range(PACK):
                z = bank([P, CHUNK], F32, "z")
                for g in range(2):
                    mx_pass(z[:], mx[("w1", g2, g)], t, mx[("x", g, c)], g == 0, g == 1)
                at = B1_AT + PACK * g2 + t
                nc.scalar.activation(
                    out=h_rows[(g2, c)][:, t, :], in_=z[:], func=ACT.Silu,
                    bias=bias_cols[:, at : at + 1], scale=1.0,
                )

        def first_layer_pair(pair, z):
            cols = slice(pair * 256, (pair + 1) * 256)
            for t in range(PACK):
                for g in range(2):
                    xw = mx[("x", g, 0)]
                    mx_pass(z[t][:, cols], mx[("w1", 0, g)], t, (xw[0][:, cols], xw[1][:, cols]), g == 0, g == 1)

        def silu_bank(g2, c, t, z):
            at = B1_AT + PACK * g2 + t
            nc.scalar.activation(
                out=h_rows[(g2, c)][:, t, :], in_=z[:], func=ACT.Silu,
                bias=bias_cols[:, at : at + 1], scale=1.0,
            )

        block_grouped = {}
        block_mx = {}

        def regroup_block(b, engine, slices):
            chunk, part = b // 2, b % 2
            if b not in block_grouped:
                block_grouped[b] = wide.tile(
                    [P, SLICES, BLOCK, PACK], BF16, name="block_grouped", tag="block_grouped", align_bytes=64
                )
            sources = [rows[("wv", chunk, g)] for g in range(2)] + [rows[("w2", chunk, g)] for g in range(3)]
            for s in slices:
                if engine == "tensor":
                    regroup_by_tensor(
                        block_grouped[b][:, s, :, :], sources[s][:, :, part * BLOCK : (part + 1) * BLOCK]
                    )
                    continue
                side_by_side(
                    engine,
                    block_grouped[b][:, s, :, :],
                    sources[s][:, :, part * BLOCK : (part + 1) * BLOCK],
                )

        def quantise_block(b):
            quantise_slices(b, ((0, 4), (4, 5)))

        def quantise_slices(b, parts):
            grouped = block_grouped[b]
            if b in block_mx:
                words, scales = block_mx[b]
            else:
                words = keep.tile([P, SLICES, BLOCK], U32, name="words_block_%d" % b, align_bytes=256)
                scales = keep.tile([P, SLICES, BLOCK], U8, name="scales_block_%d" % b, align_bytes=256)
                block_mx[b] = (words, scales)
            for lo, hi in parts:
                nc.vector.quantize_mx(
                    out=words[:, lo:hi, :].rearrange("p s w -> p (s w)").bitcast(FP8X4),
                    scales=scales[:, lo:hi, :].rearrange("p s w -> p (s w)"),
                    in_=grouped[:, lo:hi, :, :].rearrange("p s w t -> p (s w t)"),
                )

        def wv_slice(b, g):
            return (block_mx[b][0][:, g, :], block_mx[b][1][:, g, :])

        def w2_slice(b, g):
            return (block_mx[b][0][:, 2 + g, :], block_mx[b][1][:, 2 + g, :])

        vsum, gsum, gates, products = {}, {}, {}, {}

        def pass_v(j, c):
            b, k = j // 2, j % 2
            v = vbank("v")
            for g in range(2):
                mx_pass(v[:], wv_slice(b, g), k, mx[("x", g, c)], g == 0, g == 1)
            vsum[(j, c)] = v

        def pass_g(j, c, gs=(0, 1, 2)):
            b, k = j // 2, j % 2
            if (j, c) not in gsum:
                gsum[(j, c)] = bank([P, CHUNK], F32, "gsum")
            for g in gs:
                mx_pass(gsum[(j, c)][:], w2_slice(b, g), k, mx[("h", g, c)], g == 0, g == 2)

        def gate(j, c):
            s = tail.tile([P, CHUNK], F32, name="gate", tag="gate")
            nc.scalar.activation(
                out=s[:], in_=gsum[(j, c)][:], func=ACT.Sigmoid,
                bias=bias_cols[:, B2G_AT + j : B2G_AT + j + 1], scale=1.0,
            )
            gates[(j, c)] = s

        def multiply_unit(j, c):
            prod = tail.tile([P, CHUNK], F32, name="product", tag="product", bufs=6)
            nc.vector.scalar_tensor_tensor(
                out=prod[:], in0=vsum[(j, c)][:], scalar=bias_cols[:, BV_AT + j : BV_AT + j + 1],
                in1=gates[(j, c)][:], op0=ALU.add, op1=ALU.mult,
            )
            products[(j, c)] = prod

        def back_pair(pair):
            banks = []
            for unit in pair:
                back = bank([P, 4, P], F32, "back")
                for r in range(4):
                    nc.tensor.transpose(back[:, r, :], products[unit][:, r * P : (r + 1) * P], ident_f32[:])
                banks.append(back)
            return banks

        def out_pair(pair, banks):
            j, c = pair[0]
            result = tail.tile([P, 4, 2 * P], F32, name="result", tag="result")
            for k in range(2):
                nc.scalar.copy(out=result[:, :, k * P : (k + 1) * P], in_=banks[k][:])
            nc.sync.dma_start(out=out_view[:, 4 * c : 4 * c + 4, j * P : (j + 2) * P], in_=result[:])

        def store_pair(pair):
            out_pair(pair, back_pair(pair))

        def direct_tile(c, r):
            gv = bank([P, 2, BLOCK], F32, "gv")
            for g in range(3):
                mx_pass(gv[:, 0, :], mx[("h", g, c)], r, w2_slice(DIRECT, g), g == 0, g == 2)
            for g in range(2):
                mx_pass(gv[:, 1, :], mx[("x", g, c)], r, wv_slice(DIRECT, g), g == 0, g == 1)
            biased = tail.tile([P, 2, BLOCK], F32, name="biased", tag="product", bufs=6)
            nc.vector.tensor_tensor(out=biased[:], in0=gv[:], in1=bias_free[:], op=ALU.add)
            s = tail.tile([P, BLOCK], F32, name="direct_gate", tag="gate")
            nc.scalar.activation(out=s[:], in_=biased[:, 0, :], func=ACT.Sigmoid)
            return biased, s

        def direct_last_tile(c, r):
            g_bank = bank([P, BLOCK], F32, "g_last")
            for g in range(3):
                mx_pass(g_bank[:], mx[("h", g, c)], r, w2_slice(DIRECT, g), g == 0, g == 2)
            v_bank = bank([P, BLOCK], F32, "v_last")
            for g in range(2):
                mx_pass(v_bank[:], mx[("x", g, c)], r, wv_slice(DIRECT, g), g == 0, g == 1)
            biased = tail.tile([P, 2, BLOCK], F32, name="biased", tag="product", bufs=6)
            nc.vector.tensor_tensor(out=biased[:, 0, :], in0=g_bank[:], in1=bias_free[:, 0, :], op=ALU.add)
            s = tail.tile([P, BLOCK], F32, name="direct_gate", tag="gate")
            nc.scalar.activation(out=s[:], in_=biased[:, 0, :], func=ACT.Sigmoid)
            nc.vector.tensor_tensor(out=biased[:, 1, :], in0=v_bank[:], in1=bias_free[:, 1, :], op=ALU.add)
            return biased, s

        def direct_multiply(engine, queue, c, r, tile):
            biased, s = tile
            result = tail.tile([P, BLOCK], F32, name="direct_result", tag="direct_result", bufs=8)
            engine.tensor_tensor(out=result[:], in0=biased[:, 1, :], in1=s[:], op=ALU.mult)
            queue.dma_start(out=out_view[:, 4 * c + r, direct_cols], in_=result[:])

        x_words(0)
        w1_00 = regroup("vector", rows[("w1", 0, 0)])
        xt_banks = transpose_x(0, (0,))
        x_grouped = copy_x(xt_banks)
        quantise(w1_00, ("w1", 0, 0))
        w1_01 = regroup_shared(rows[("w1", 0, 1)], 128)
        quantise_x_pair(x_grouped, 0, 0, 0)
        quantise(w1_01, ("w1", 0, 1))
        quantise_x_pair(x_grouped, 1, 0, 0)
        h_rows[(0, 0)] = keep.tile([P, PACK, CHUNK], BF16, name="h_0_0", tag="rows_w1_0_0")
        z0 = [bank([P, CHUNK], F32, "z") for t in range(PACK)]
        xt_banks = transpose_x(0, (1,))
        bias_t = bank([P, P], BF16, "bias_t")
        nc.tensor.transpose(bias_t[:], bias_rows[:], ident_bf16[:])
        bias_cols = const.tile([P, 32], F32, name="bias_cols")
        copy_x(xt_banks, x_grouped)
        first_layer_pair(0, z0)
        w1_10 = regroup_shared(rows[("w1", 1, 0)], 256)
        quantise_x_pair(x_grouped, 0, 0, 1)
        quantise_x_pair(x_grouped, 1, 0, 1)
        nc.vector.tensor_copy(out=bias_cols[:, 0:BIAS_TILES], in_=bias_t[:, 0:BIAS_TILES])
        first_layer_pair(1, z0)
        for t in range(PACK):
            silu_bank(0, 0, t, z0[t])
        w1_11 = regroup("vector", rows[("w1", 1, 1)])
        quantise(w1_10, ("w1", 1, 0))
        quantise(w1_11, ("w1", 1, 1))
        first_layer(1, 0)
        w1_20 = regroup("vector", rows[("w1", 2, 0)])
        w1_21 = regroup("vector", rows[("w1", 2, 1)])
        quantise(w1_20, ("w1", 2, 0))
        quantise(w1_21, ("w1", 2, 1))
        x_grouped = copy_x(transpose_x(1))
        first_layer(2, 0)
        h_00 = regroup("vector", h_rows[(0, 0)])
        quantise(x_grouped[0], ("x", 0, 1))
        quantise(x_grouped[1], ("x", 1, 1))
        first_layer(0, 1)
        h_10 = regroup("vector", h_rows[(1, 0)])
        quantise(h_00, ("h", 0, 0))
        regroup_block(0, "vector", (0, 1))
        first_layer(1, 1)
        quantise(h_10, ("h", 1, 0))
        h_20 = regroup("vector", h_rows[(2, 0)])
        regroup_block(0, "vector", (2, 3))
        quantise(h_20, ("h", 2, 0))
        regroup_block(0, "vector", (4,))
        quantise_block(0)
        first_layer(2, 1)
        regroup_block(1, "tensor", (0, 1))
        nc.scalar.activation(out=warm[:, 2:3], in_=h_rows[(2, 1)][:, 3, 0:1], func=ACT.Sigmoid)
        for j in range(2):
            pass_v(j, 0)
            pass_g(j, 0)
            gate(j, 0)
        h_01 = regroup("vector", h_rows[(0, 1)])
        regroup_block(1, "vector", (2, 3, 4))
        for j in range(2):
            pass_v(j, 1)
        quantise_block(1)
        quantise(h_01, ("h", 0, 1))
        multiply_unit(0, 0)
        h_11 = regroup_shared(h_rows[(1, 1)], 256)
        multiply_unit(1, 0)
        h_21 = regroup_shared(h_rows[(2, 1)], 256)
        for j in range(2, 4):
            pass_v(j, 0)
            pass_g(j, 0)
            gate(j, 0)
        quantise(h_11, ("h", 1, 1))
        regroup_block(2, "scalar", (0,))
        store_pair([(0, 0), (1, 0)])
        for j in range(2):
            pass_g(j, 1, (0, 1))
        multiply_unit(2, 0)
        quantise(h_21, ("h", 2, 1))
        multiply_unit(3, 0)
        for j in range(2):
            pass_g(j, 1, (2,))
            gate(j, 1)
        store_pair([(2, 0), (3, 0)])
        regroup_block(2, "vector", (1, 2, 3, 4))
        for j in range(2):
            multiply_unit(j, 1)
        quantise_block(2)
        for j in range(2, 4):
            pass_v(j, 1)
            pass_g(j, 1)
            gate(j, 1)
        store_pair([(0, 1), (1, 1)])
        multiply_unit(2, 1)
        multiply_unit(3, 1)
        for j in range(4, 6):
            pass_v(j, 0)
            pass_g(j, 0)
            gate(j, 0)
        regroup_block(3, "scalar", (0,))
        regroup_block(3, "vector", (1, 2, 3, 4))
        multiply_unit(4, 0)
        multiply_unit(5, 0)
        quantise_block(3)
        for j in range(4, 6):
            pass_v(j, 1)
            pass_g(j, 1)
            gate(j, 1)
        stores = [back_pair([(2, 1), (3, 1)]), back_pair([(4, 0), (5, 0)])]
        out_pair([(2, 1), (3, 1)], stores[0])
        out_pair([(4, 0), (5, 0)], stores[1])
        multiply_unit(4, 1)
        multiply_unit(5, 1)
        tiles = [direct_tile(0, r) for r in range(4)]
        for r in range(4):
            direct_multiply(nc.gpsimd, nc.sync, 0, r, tiles[r])
        store_pair([(4, 1), (5, 1)])
        tiles = [direct_tile(1, r) for r in range(3)]
        for r in range(2):
            direct_multiply(nc.gpsimd, nc.sync, 1, r, tiles[r])
        last = direct_last_tile(1, 3)
        direct_multiply(nc.vector, nc.sync, 1, 2, tiles[2])
        direct_multiply(nc.vector, nc.sync, 1, 3, last)
